import numpy as np
import ml_dtypes


def mxq(x, axis, fmt="e4m3"):
    dtype, down = {"e4m3": (ml_dtypes.float8_e4m3fn, 7), "e5m2": (ml_dtypes.float8_e5m2, 14)}[fmt]
    v = np.moveaxis(np.asarray(x, np.float32).astype(ml_dtypes.bfloat16).astype(np.float64), axis, -1)
    blocks = v.reshape(v.shape[:-1] + (-1, 32))
    amax = np.abs(blocks).max(-1, keepdims=True)
    byte = np.maximum(np.where(amax > 0, np.frexp(amax)[1] - 1 + 127, 0) - down, 1)
    scale = np.exp2(byte - 127.0)
    codes = (blocks / scale).astype(np.float32).astype(dtype).astype(np.float64)
    return np.moveaxis((codes * scale).reshape(v.shape), -1, axis)


WIDE = False


def mx_kscale(k):
    if not WIDE:
        return np.ones(k)
    levels = np.array([10, -10, 5, -5, 0])
    a = np.random.permutation(np.resize(levels, k // 512 * 4)).reshape(k // 512, 4)
    idx = np.arange(k)
    return np.exp2(a[idx // 512, idx % 128 // 32])


BF16 = ml_dtypes.bfloat16


def bf(x):
    return np.asarray(x, np.float32).astype(BF16)


def f64(x):
    return np.asarray(x).astype(np.float64)


B, S, D, H, QL, KVL, RD, ND, VD = 2, 256, 2048, 16, 1536, 512, 128, 64, 128
ROPE_THETA, ROPE_RATIO = 10000.0, 1.0


def rope_tables(seq_len):
    half = RD // 2
    inv_freq = ROPE_RATIO / (ROPE_THETA ** (np.arange(half) * 2.0 / RD))
    freqs = np.arange(seq_len)[:, None] * inv_freq[None, :]
    return np.cos(freqs), np.sin(freqs)


def apply_rope(x, cos, sin):
    x_even = x[..., 0::2]
    x_odd = x[..., 1::2]
    r_even = x_even * cos - x_odd * sin
    r_odd = x_odd * cos + x_even * sin
    return np.stack([r_even, r_odd], axis=-1).reshape(x.shape)


def setup_inputs():
    s, t = mx_kscale(D), mx_kscale(KVL)
    tc = np.concatenate([t, np.ones(RD)])
    return {"hidden_states": bf(np.random.standard_normal((B, S, D)) * s),
            "Wkva": bf(np.random.standard_normal((D, KVL + RD)) / np.sqrt(D) / s[:, None] * tc),
            "Wkvb": bf(np.random.standard_normal((KVL, H * (ND + VD))) / np.sqrt(KVL) / t[:, None])}


def reference(hidden_states, Wkva, Wkvb):
    kv_comp = mxq(f64(hidden_states), 2, "e4m3") @ mxq(f64(Wkva), 0, "e4m3")
    c_kv, k_pe = kv_comp[..., :KVL], kv_comp[..., KVL:]
    cos, sin = rope_tables(S)
    k_pe = apply_rope(k_pe, cos, sin)
    kv = (mxq(c_kv, 2, "e4m3") @ mxq(f64(Wkvb), 0, "e4m3")).reshape(B, S, H, ND + VD)
    kv = kv.transpose(0, 2, 1, 3)
    k_nope, v = kv[..., :ND], kv[..., ND:]
    k_pe_b = np.broadcast_to(k_pe[:, None], (B, H, S, RD))
    k_full = np.concatenate([k_nope, k_pe_b], axis=-1)
    return k_full, v

@@ -1,0 +1,322 @@
+import math
+from contextlib import ExitStack
+
+import concourse.mybir as mybir
+from concourse.masks import make_identity
+
+F32 = mybir.dt.float32
+BF16 = mybir.dt.bfloat16
+I32 = mybir.dt.int32
+U32 = mybir.dt.uint32
+U8 = mybir.dt.uint8
+FP8X4 = mybir.dt.float8_e4m3fn_x4
+ALU = mybir.AluOpType
+ACT = mybir.ActivationFunctionType
+
+P = 128
+PACK = 4
+K_PASS = P * PACK
+
+B, S, D, H = 2, 256, 2048, 16
+KVL, RD, ND, VD = 512, 128, 64, 128
+ROPE_THETA = 10000.0
+
+TOKENS = B * S
+POS_PER_PART = S // P
+CHUNKS = B * POS_PER_PART
+PASSES = D // K_PASS
+WA_COLS = KVL + RD
+HEAD_COLS = ND + VD
+GROUP_HEADS = 4
+GROUPS = H // GROUP_HEADS
+GROUP_COLS = GROUP_HEADS * HEAD_COLS
+HALF = RD // 2
+RUN = 4
+ROUND_MAGIC = 1.5 * 2.0**23
+
+FLOPS = 2 * TOKENS * D * WA_COLS + 2 * TOKENS * KVL * H * HEAD_COLS
+
+
+def regroup(nc, grouped, rows):
+    width = rows.shape[2]
+    split = 64 * round(width * 2 / (3 * 64))
+    nc.vector.tensor_copy(
+        out=grouped[:, 0:split, :].rearrange("p (c i) t -> p c t i", i=RUN),
+        in_=rows[:, :, 0:split].rearrange("p t (c i) -> p c t i", i=RUN),
+    )
+    nc.scalar.copy(
+        out=grouped[:, split:width, :].rearrange("p (c i) t -> p c t i", i=RUN),
+        in_=rows[:, :, split:width].rearrange("p t (c i) -> p c t i", i=RUN),
+    )
+
+
+def quantise(nc, codes, scales, grouped):
+    nc.vector.quantize_mx(
+        out=codes.bitcast(FP8X4),
+        scales=scales,
+        in_=grouped.rearrange("p w t -> p (w t)"),
+    )
+
+
+def tile_mlaattention_pb_kernel(tc, hidden_states, Wkva, Wkvb, k_full, v):
+    nc = tc.nc
+    with ExitStack() as stack:
+        keep = stack.enter_context(tc.tile_pool(name="keep", bufs=1))
+        stage = stack.enter_context(tc.tile_pool(name="stage", bufs=2))
+        x_stage = stack.enter_context(tc.tile_pool(name="x_stage", bufs=4))
+        per_group = stack.enter_context(tc.tile_pool(name="per_group", bufs=GROUPS))
+        outs = stack.enter_context(tc.tile_pool(name="outs", bufs=3))
+        banks = stack.enter_context(tc.psum_pool(name="banks", bufs=8))
+        stack.enter_context(tc.manual_schedule())
+
+        x_sb = keep.tile([P, B, POS_PER_PART, D], BF16)
+        for b in range(B):
+            nc.sync.dma_start(
+                out=x_sb[:, b],
+                in_=hidden_states[b].rearrange("(p e) k -> p e k", e=POS_PER_PART),
+            )
+        wa_raw = keep.tile([P, PASSES, 2, 2 * WA_COLS], BF16)
+        for g in range(PASSES):
+            nc.sync.dma_start(
+                out=wa_raw[:, g],
+                in_=Wkva[g * K_PASS : (g + 1) * K_PASS, :].rearrange(
+                    "(u q e) c -> q u (e c)", u=2, e=2
+                ),
+            )
+        wb_raw = keep.tile([P, GROUPS, PACK, GROUP_COLS], BF16)
+        for hg in range(GROUPS):
+            nc.sync.dma_start(
+                out=wb_raw[:, hg],
+                in_=Wkvb[:, hg * GROUP_COLS : (hg + 1) * GROUP_COLS].rearrange(
+                    "(t p) n -> p t n", p=P
+                ),
+            )
+
+        ident = keep.tile([P, P], F32)
+        make_identity(nc, ident[:])
+        pos = keep.tile([P, B, POS_PER_PART], I32)
+        nc.gpsimd.iota(
+            pos[:], pattern=[[0, B], [1, POS_PER_PART]], base=0, channel_multiplier=POS_PER_PART
+        )
+        turns = keep.tile([P, 2, CHUNKS, HALF], F32)
+        nc.vector.tensor_scalar(
+            out=turns[:, 1, :, 0:1],
+            in0=pos[:].rearrange("p b e -> p (b e)").unsqueeze(2),
+            scalar1=1.0 / (2.0 * math.pi),
+            scalar2=None,
+            op0=ALU.mult,
+        )
+        ratio = ROPE_THETA ** (-2.0 / RD)
+        width = 1
+        while width < HALF:
+            nc.vector.tensor_scalar(
+                out=turns[:, 1, :, width : 2 * width],
+                in0=turns[:, 1, :, 0:width],
+                scalar1=ratio**width,
+                scalar2=None,
+                op0=ALU.mult,
+            )
+            width *= 2
+        nc.vector.tensor_scalar(
+            out=turns[:, 0], in0=turns[:, 1], scalar1=0.25, scalar2=None, op0=ALU.add
+        )
+        whole = keep.tile([P, 2, CHUNKS, HALF], F32)
+        nc.vector.tensor_scalar(
+            out=whole[:],
+            in0=turns[:],
+            scalar1=ROUND_MAGIC,
+            scalar2=ROUND_MAGIC,
+            op0=ALU.add,
+            op1=ALU.subtract,
+        )
+        nc.vector.tensor_tensor(out=whole[:], in0=turns[:], in1=whole[:], op=ALU.subtract)
+        cos_sin = keep.tile([P, 2, CHUNKS, HALF], F32)
+        nc.scalar.activation(out=cos_sin[:], in_=whole[:], func=ACT.Sin, scale=2.0 * math.pi)
+
+        xt_banks = []
+        for b in range(B):
+            for g in range(PASSES):
+                xt = banks.tile([P, 2, S], F32, tag="bank")
+                for u in range(2):
+                    for e in range(POS_PER_PART):
+                        first = (2 * g + u) * P
+                        nc.tensor.transpose(
+                            out=xt[:, u, e * P : (e + 1) * P],
+                            in_=x_sb[:, b, e, :].bitcast(F32)[:, first : first + P],
+                            identity=ident[:],
+                        )
+                xt_banks.append(xt)
+        x_codes = keep.tile([P, PASSES, TOKENS], U32, align_bytes=64)
+        x_scales = keep.tile([P, PASSES, TOKENS], U8, align_bytes=64)
+        for b in range(B):
+            batch_cols = slice(b * S, (b + 1) * S)
+            for g in range(PASSES):
+                xt = xt_banks[b * PASSES + g]
+                x_grouped = x_stage.tile([P, S, PACK], BF16, align_bytes=64)
+                if g % 2 == 0:
+                    nc.scalar.copy(
+                        out=x_grouped[:].bitcast(F32), in_=xt[:].rearrange("q u w -> q w u")
+                    )
+                else:
+                    nc.vector.tensor_copy(
+                        out=x_grouped[:].bitcast(F32), in_=xt[:].rearrange("q u w -> q w u")
+                    )
+                quantise(nc, x_codes[:, g, batch_cols], x_scales[:, g, batch_cols], x_grouped[:])
+
+        wa_codes = keep.tile([P, PASSES, KVL], U32, align_bytes=64)
+        wa_scales = keep.tile([P, PASSES, KVL], U8, align_bytes=64)
+        ckv_acc = [
+            banks.tile([P, TOKENS], F32, tag="bank", name="ckv_acc%d" % m) for m in range(PACK)
+        ]
+        for g in range(PASSES):
+            wa_rows = wa_raw[:, g].rearrange("p u (e c) -> p (u e) c", e=2)
+            wa_grouped = stage.tile([P, KVL, PACK], BF16, align_bytes=64)
+            regroup(nc, wa_grouped, wa_rows[:, :, 0:KVL])
+            quantise(nc, wa_codes[:, g, :], wa_scales[:, g, :], wa_grouped[:])
+            for m in range(PACK):
+                latent = slice(m * P, (m + 1) * P)
+                nc.tensor.matmul_mx(
+                    out=ckv_acc[m][:],
+                    lhsT=wa_codes[:, g, latent].bitcast(FP8X4),
+                    lhsT_scale=wa_scales[:, g, latent],
+                    rhs=x_codes[:, g, :].bitcast(FP8X4),
+                    rhs_scale=x_scales[:, g, :],
+                    start=(g == 0),
+                    stop=(g == PASSES - 1),
+                )
+
+        def quantised_weights(hg, first, size):
+            heads = wb_raw[:, hg].rearrange("p t (h d) -> p t h d", h=GROUP_HEADS)
+            grouped = stage.tile([P, GROUP_HEADS * size, PACK], BF16, align_bytes=64, tag="wb%d" % size)
+            nc.vector.tensor_copy(
+                out=grouped[:].rearrange("p (h c i) t -> p h c t i", h=GROUP_HEADS, i=RUN),
+                in_=heads[:, :, :, first : first + size].rearrange("p t h (c i) -> p h c t i", i=RUN),
+            )
+            codes = per_group.tile([P, GROUP_HEADS * size], U32, align_bytes=64, tag="codes%d" % size)
+            scales = per_group.tile([P, GROUP_HEADS * size], U8, align_bytes=64, tag="scales%d" % size)
+            quantise(nc, codes[:], scales[:], grouped[:])
+            return codes, scales
+
+        wv_next = quantised_weights(0, ND, VD)
+
+        ckv_rows = keep.tile([P, PACK, TOKENS], BF16)
+        for m in range(PACK):
+            nc.scalar.copy(out=ckv_rows[:, m, :], in_=ckv_acc[m][:])
+        ckv_grouped = keep.tile([P, TOKENS, PACK], BF16, align_bytes=64)
+        ckv_codes = keep.tile([P, TOKENS], U32, align_bytes=64)
+        ckv_scales = keep.tile([P, TOKENS], U8, align_bytes=64)
+        for b in range(B):
+            batch_cols = slice(b * S, (b + 1) * S)
+            regroup(nc, ckv_grouped[:, batch_cols, :], ckv_rows[:, :, batch_cols])
+            quantise(
+                nc, ckv_codes[:, batch_cols], ckv_scales[:, batch_cols], ckv_grouped[:, batch_cols, :]
+            )
+
+        def second_matmul(out, c, weights):
+            codes, scales = weights
+            tokens = slice(c * P, (c + 1) * P)
+            nc.tensor.matmul_mx(
+                out=out,
+                lhsT=ckv_codes[:, tokens].bitcast(FP8X4),
+                lhsT_scale=ckv_scales[:, tokens],
+                rhs=codes[:].bitcast(FP8X4),
+                rhs_scale=scales[:],
+                start=True,
+                stop=True,
+            )
+
+        for hg in range(GROUPS):
+            group_heads = slice(hg * GROUP_HEADS, (hg + 1) * GROUP_HEADS)
+            wv = wv_next
+            if hg + 1 < GROUPS:
+                wv_next = quantised_weights(hg + 1, ND, VD)
+            v_out = outs.tile([P, B, GROUP_HEADS, POS_PER_PART, VD], F32)
+            for b in range(B):
+                for e in range(POS_PER_PART):
+                    v_ps = banks.tile([P, GROUP_HEADS * VD], F32, tag="bank")
+                    second_matmul(v_ps[:], b * POS_PER_PART + e, wv)
+                    nc.scalar.copy(
+                        out=v_out[:, b, :, e, :],
+                        in_=v_ps[:].rearrange("p (h d) -> p h d", h=GROUP_HEADS),
+                    )
+                nc.sync.dma_start(
+                    out=v[b, group_heads].rearrange("h (p e) d -> p h (e d)", e=POS_PER_PART),
+                    in_=v_out[:, b].rearrange("p h e d -> p h (e d)"),
+                )
+
+        wr_grouped = keep.tile([P, PASSES, RD, PACK], BF16, align_bytes=64)
+        nc.vector.tensor_copy(
+            out=wr_grouped[:].rearrange("p g (c i) t -> p g c t i", i=RUN),
+            in_=wa_raw[:]
+            .rearrange("p g u (e c) -> p g (u e) c", e=2)[:, :, :, KVL:]
+            .rearrange("p g t (c i) -> p g c t i", i=RUN),
+        )
+        wr_codes = keep.tile([P, PASSES, RD], U32, align_bytes=64)
+        wr_scales = keep.tile([P, PASSES, RD], U8, align_bytes=64)
+        nc.vector.quantize_mx(
+            out=wr_codes[:].rearrange("p g c -> p (g c)").bitcast(FP8X4),
+            scales=wr_scales[:].rearrange("p g c -> p (g c)"),
+            in_=wr_grouped[:].rearrange("p g c t -> p (g c t)"),
+        )
+        kpe_ps = banks.tile([P, CHUNKS, RD], F32, tag="bank")
+        for c in range(CHUNKS):
+            tokens = slice(c * P, (c + 1) * P)
+            for g in range(PASSES):
+                nc.tensor.matmul_mx(
+                    out=kpe_ps[:, c, :],
+                    lhsT=x_codes[:, g, tokens].bitcast(FP8X4),
+                    lhsT_scale=x_scales[:, g, tokens],
+                    rhs=wr_codes[:, g, :].bitcast(FP8X4),
+                    rhs_scale=wr_scales[:, g, :],
+                    start=(g == 0),
+                    stop=(g == PASSES - 1),
+                )
+        wk_next = quantised_weights(0, 0, ND)
+
+        kpe_pairs = kpe_ps[:].rearrange("p c (i j) -> p j c i", j=2)
+        table_shape = [P, 2, CHUNKS, HALF]
+        by_cos = keep.tile(table_shape, F32)
+        by_sin = keep.tile(table_shape, F32)
+        nc.vector.tensor_tensor(
+            out=by_cos[:],
+            in0=kpe_pairs,
+            in1=cos_sin[:, 0].unsqueeze(1).to_broadcast(table_shape),
+            op=ALU.mult,
+        )
+        nc.vector.tensor_tensor(
+            out=by_sin[:],
+            in0=kpe_pairs,
+            in1=cos_sin[:, 1].unsqueeze(1).to_broadcast(table_shape),
+            op=ALU.mult,
+        )
+        kpe_rot = keep.tile([P, CHUNKS, RD], F32)
+        rot_pairs = kpe_rot[:].rearrange("p c (i j) -> p j c i", j=2)
+        nc.vector.tensor_tensor(
+            out=rot_pairs[:, 0], in0=by_cos[:, 0], in1=by_sin[:, 1], op=ALU.subtract
+        )
+        nc.vector.tensor_tensor(out=rot_pairs[:, 1], in0=by_cos[:, 1], in1=by_sin[:, 0], op=ALU.add)
+
+        for hg in range(GROUPS):
+            group_heads = slice(hg * GROUP_HEADS, (hg + 1) * GROUP_HEADS)
+            wk = wk_next
+            k_out = outs.tile([P, B, GROUP_HEADS, POS_PER_PART, HEAD_COLS], F32)
+            for b in range(B):
+                k_ps = banks.tile([P, POS_PER_PART, GROUP_HEADS * ND], F32, tag="bank")
+                for e in range(POS_PER_PART):
+                    second_matmul(k_ps[:, e, :], b * POS_PER_PART + e, wk)
+                nc.scalar.copy(
+                    out=k_out[:, b, :, :, 0:ND].rearrange("p h e d -> p e h d"),
+                    in_=k_ps[:].rearrange("p e (h d) -> p e h d", h=GROUP_HEADS),
+                )
+                nc.vector.tensor_copy(
+                    out=k_out[:, b, :, :, ND:],
+                    in_=kpe_rot[:, b * POS_PER_PART : (b + 1) * POS_PER_PART, :]
+                    .unsqueeze(1)
+                    .to_broadcast([P, GROUP_HEADS, POS_PER_PART, RD]),
+                )
+                nc.sync.dma_start(
+                    out=k_full[b, group_heads].rearrange("h (p e) d -> p h (e d)", e=POS_PER_PART),
+                    in_=k_out[:, b].rearrange("p h e d -> p h (e d)"),
+                )
+            if hg + 1 < GROUPS:
+                wk_next = quantised_weights(hg + 1, 0, ND)

@@ -32,21 +32,16 @@ GROUPS = H // GROUP_HEADS
 GROUP_COLS = GROUP_HEADS * HEAD_COLS
 HALF = RD // 2
 RUN = 4
+WA_VECTOR_COLS = 320
 ROUND_MAGIC = 1.5 * 2.0**23
 
 FLOPS = 2 * TOKENS * D * WA_COLS + 2 * TOKENS * KVL * H * HEAD_COLS
 
 
-def regroup(nc, grouped, rows):
-    width = rows.shape[2]
-    split = 64 * round(width * 2 / (3 * 64))
-    nc.vector.tensor_copy(
-        out=grouped[:, 0:split, :].rearrange("p (c i) t -> p c t i", i=RUN),
-        in_=rows[:, :, 0:split].rearrange("p t (c i) -> p c t i", i=RUN),
-    )
-    nc.scalar.copy(
-        out=grouped[:, split:width, :].rearrange("p (c i) t -> p c t i", i=RUN),
-        in_=rows[:, :, split:width].rearrange("p t (c i) -> p c t i", i=RUN),
+def regroup(copy, grouped, rows):
+    copy(
+        out=grouped.rearrange("p (c i) t -> p c t i", i=RUN),
+        in_=rows.rearrange("p t (c i) -> p c t i", i=RUN),
     )
 
 
@@ -148,42 +143,59 @@ def tile_mlaattention_pb_kernel(tc, hidden_states, Wkva, Wkvb, k_full, v):
                 xt_banks.append(xt)
         x_codes = keep.tile([P, PASSES, TOKENS], U32, align_bytes=64)
         x_scales = keep.tile([P, PASSES, TOKENS], U8, align_bytes=64)
-        for b in range(B):
+
+        def quantise_x(b, g):
             batch_cols = slice(b * S, (b + 1) * S)
-            for g in range(PASSES):
-                xt = xt_banks[b * PASSES + g]
-                x_grouped = x_stage.tile([P, S, PACK], BF16, align_bytes=64)
-                if g % 2 == 0:
-                    nc.scalar.copy(
-                        out=x_grouped[:].bitcast(F32), in_=xt[:].rearrange("q u w -> q w u")
-                    )
-                else:
-                    nc.vector.tensor_copy(
-                        out=x_grouped[:].bitcast(F32), in_=xt[:].rearrange("q u w -> q w u")
-                    )
-                quantise(nc, x_codes[:, g, batch_cols], x_scales[:, g, batch_cols], x_grouped[:])
+            x_grouped = x_stage.tile([P, S, PACK], BF16, align_bytes=64)
+            nc.scalar.copy(
+                out=x_grouped[:].bitcast(F32),
+                in_=xt_banks[b * PASSES + g][:].rearrange("q u w -> q w u"),
+            )
+            quantise(nc, x_codes[:, g, batch_cols], x_scales[:, g, batch_cols], x_grouped[:])
 
         wa_codes = keep.tile([P, PASSES, KVL], U32, align_bytes=64)
         wa_scales = keep.tile([P, PASSES, KVL], U8, align_bytes=64)
-        ckv_acc = [
-            banks.tile([P, TOKENS], F32, tag="bank", name="ckv_acc%d" % m) for m in range(PACK)
-        ]
         for g in range(PASSES):
+            quantise_x(0, g)
+        for g in range(PASSES):
+            quantise_x(1, g)
             wa_rows = wa_raw[:, g].rearrange("p u (e c) -> p (u e) c", e=2)
             wa_grouped = stage.tile([P, KVL, PACK], BF16, align_bytes=64)
-            regroup(nc, wa_grouped, wa_rows[:, :, 0:KVL])
+            regroup(
+                nc.vector.tensor_copy,
+                wa_grouped[:, 0:WA_VECTOR_COLS, :],
+                wa_rows[:, :, 0:WA_VECTOR_COLS],
+            )
+            regroup(
+                nc.scalar.copy,
+                wa_grouped[:, WA_VECTOR_COLS:, :],
+                wa_rows[:, :, WA_VECTOR_COLS:KVL],
+            )
             quantise(nc, wa_codes[:, g, :], wa_scales[:, g, :], wa_grouped[:])
-            for m in range(PACK):
-                latent = slice(m * P, (m + 1) * P)
-                nc.tensor.matmul_mx(
-                    out=ckv_acc[m][:],
-                    lhsT=wa_codes[:, g, latent].bitcast(FP8X4),
-                    lhsT_scale=wa_scales[:, g, latent],
-                    rhs=x_codes[:, g, :].bitcast(FP8X4),
-                    rhs_scale=x_scales[:, g, :],
-                    start=(g == 0),
-                    stop=(g == PASSES - 1),
-                )
+
+        ckv_acc = [
+            [banks.tile([P, S], F32, tag="bank", name="ckv_acc%d%d" % (b, m)) for m in range(PACK)]
+            for b in range(B)
+        ]
+        for g in range(PASSES):
+            for b in range(B):
+                batch_cols = slice(b * S, (b + 1) * S)
+                for m in range(PACK):
+                    latent = slice(m * P, (m + 1) * P)
+                    nc.tensor.matmul_mx(
+                        out=ckv_acc[b][m][:],
+                        lhsT=wa_codes[:, g, latent].bitcast(FP8X4),
+                        lhsT_scale=wa_scales[:, g, latent],
+                        rhs=x_codes[:, g, batch_cols].bitcast(FP8X4),
+                        rhs_scale=x_scales[:, g, batch_cols],
+                        start=(g == 0),
+                        stop=(g == PASSES - 1),
+                    )
+
+        wr_grouped = keep.tile([P, PASSES, RD, PACK], BF16, align_bytes=64)
+        for g in range(PASSES):
+            wa_rows = wa_raw[:, g].rearrange("p u (e c) -> p (u e) c", e=2)
+            regroup(nc.scalar.copy, wr_grouped[:, g], wa_rows[:, :, KVL:])
 
         def quantised_weights(hg, first, size):
             heads = wb_raw[:, hg].rearrange("p t (h d) -> p t h d", h=GROUP_HEADS)
@@ -200,14 +212,14 @@ def tile_mlaattention_pb_kernel(tc, hidden_states, Wkva, Wkvb, k_full, v):
         wv_next = quantised_weights(0, ND, VD)
 
         ckv_rows = keep.tile([P, PACK, TOKENS], BF16)
-        for m in range(PACK):
-            nc.scalar.copy(out=ckv_rows[:, m, :], in_=ckv_acc[m][:])
         ckv_grouped = keep.tile([P, TOKENS, PACK], BF16, align_bytes=64)
         ckv_codes = keep.tile([P, TOKENS], U32, align_bytes=64)
         ckv_scales = keep.tile([P, TOKENS], U8, align_bytes=64)
         for b in range(B):
             batch_cols = slice(b * S, (b + 1) * S)
-            regroup(nc, ckv_grouped[:, batch_cols, :], ckv_rows[:, :, batch_cols])
+            for m in range(PACK):
+                nc.scalar.copy(out=ckv_rows[:, m, batch_cols], in_=ckv_acc[b][m][:])
+            regroup(nc.vector.tensor_copy, ckv_grouped[:, batch_cols, :], ckv_rows[:, :, batch_cols])
             quantise(
                 nc, ckv_codes[:, batch_cols], ckv_scales[:, batch_cols], ckv_grouped[:, batch_cols, :]
             )
@@ -244,13 +256,6 @@ def tile_mlaattention_pb_kernel(tc, hidden_states, Wkva, Wkvb, k_full, v):
                     in_=v_out[:, b].rearrange("p h e d -> p h (e d)"),
                 )
 
-        wr_grouped = keep.tile([P, PASSES, RD, PACK], BF16, align_bytes=64)
-        nc.vector.tensor_copy(
-            out=wr_grouped[:].rearrange("p g (c i) t -> p g c t i", i=RUN),
-            in_=wa_raw[:]
-            .rearrange("p g u (e c) -> p g (u e) c", e=2)[:, :, :, KVL:]
-            .rearrange("p g t (c i) -> p g c t i", i=RUN),
-        )
         wr_codes = keep.tile([P, PASSES, RD], U32, align_bytes=64)
         wr_scales = keep.tile([P, PASSES, RD], U8, align_bytes=64)
         nc.vector.quantize_mx(

@@ -22,8 +22,10 @@ KVL, RD, ND, VD = 512, 128, 64, 128
 ROPE_THETA = 10000.0
 
 TOKENS = B * S
-POS_PER_PART = S // P
-CHUNKS = B * POS_PER_PART
+CHUNKS = TOKENS // P
+HALVES = 2
+HALF_CHUNKS = CHUNKS // HALVES
+HALF_TOKENS = HALF_CHUNKS * P
 PASSES = D // K_PASS
 WA_COLS = KVL + RD
 HEAD_COLS = ND + VD
@@ -64,12 +66,15 @@ def tile_mlaattention_pb_kernel(tc, hidden_states, Wkva, Wkvb, k_full, v):
         banks = stack.enter_context(tc.psum_pool(name="banks", bufs=8))
         stack.enter_context(tc.manual_schedule())
 
-        x_sb = keep.tile([P, B, POS_PER_PART, D], BF16)
-        for b in range(B):
-            nc.sync.dma_start(
-                out=x_sb[:, b],
-                in_=hidden_states[b].rearrange("(p e) k -> p e k", e=POS_PER_PART),
-            )
+        x_sb = keep.tile([P, HALVES, HALF_CHUNKS, D], BF16)
+        for hf in range(HALVES):
+            for b in range(B):
+                nc.sync.dma_start(
+                    out=x_sb[b:P:B, hf],
+                    in_=hidden_states[b].rearrange(
+                        "(q hf e) k -> hf q e k", hf=HALVES, e=HALF_CHUNKS
+                    )[hf],
+                )
         wa_raw = keep.tile([P, PASSES, 2, 2 * WA_COLS], BF16)
         for g in range(PASSES):
             nc.sync.dma_start(
@@ -89,17 +94,28 @@ def tile_mlaattention_pb_kernel(tc, hidden_states, Wkva, Wkvb, k_full, v):
 
         ident = keep.tile([P, P], F32)
         make_identity(nc, ident[:])
-        pos = keep.tile([P, B, POS_PER_PART], I32)
-        nc.gpsimd.iota(
-            pos[:], pattern=[[0, B], [1, POS_PER_PART]], base=0, channel_multiplier=POS_PER_PART
+        first_pos = keep.tile([P, 1], I32)
+        nc.gpsimd.iota(first_pos[:], pattern=[[0, 1]], base=0, channel_multiplier=1)
+        chunk_no = keep.tile([P, CHUNKS], I32)
+        nc.gpsimd.iota(chunk_no[:], pattern=[[1, CHUNKS]], base=0, channel_multiplier=0)
+        nc.vector.tensor_scalar(
+            out=first_pos[:],
+            in0=first_pos[:],
+            scalar1=1,
+            scalar2=2,
+            op0=ALU.logical_shift_right,
+            op1=ALU.logical_shift_left,
         )
+        first_pos_f = keep.tile([P, 1], F32)
+        nc.vector.tensor_copy(out=first_pos_f[:], in_=first_pos[:])
         turns = keep.tile([P, 2, CHUNKS, HALF], F32)
         nc.vector.tensor_scalar(
             out=turns[:, 1, :, 0:1],
-            in0=pos[:].rearrange("p b e -> p (b e)").unsqueeze(2),
-            scalar1=1.0 / (2.0 * math.pi),
-            scalar2=None,
-            op0=ALU.mult,
+            in0=chunk_no[:].unsqueeze(2),
+            scalar1=first_pos_f[:, 0:1],
+            scalar2=1.0 / (2.0 * math.pi),
+            op0=ALU.add,
+            op1=ALU.mult,
         )
         ratio = ROPE_THETA ** (-2.0 / RD)
         width = 1
@@ -129,29 +145,29 @@ def tile_mlaattention_pb_kernel(tc, hidden_states, Wkva, Wkvb, k_full, v):
         nc.scalar.activation(out=cos_sin[:], in_=whole[:], func=ACT.Sin, scale=2.0 * math.pi)
 
         xt_banks = []
-        for b in range(B):
+        for hf in range(HALVES):
             for g in range(PASSES):
-                xt = banks.tile([P, 2, S], F32, tag="bank")
+                xt = banks.tile([P, 2, HALF_TOKENS], F32, tag="bank")
                 for u in range(2):
-                    for e in range(POS_PER_PART):
+                    for e in range(HALF_CHUNKS):
                         first = (2 * g + u) * P
                         nc.tensor.transpose(
                             out=xt[:, u, e * P : (e + 1) * P],
-                            in_=x_sb[:, b, e, :].bitcast(F32)[:, first : first + P],
+                            in_=x_sb[:, hf, e, :].bitcast(F32)[:, first : first + P],
                             identity=ident[:],
                         )
                 xt_banks.append(xt)
         x_codes = keep.tile([P, PASSES, TOKENS], U32, align_bytes=64)
         x_scales = keep.tile([P, PASSES, TOKENS], U8, align_bytes=64)
 
-        def quantise_x(b, g):
-            batch_cols = slice(b * S, (b + 1) * S)
-            x_grouped = x_stage.tile([P, S, PACK], BF16, align_bytes=64)
+        def quantise_x(hf, g):
+            half_cols = slice(hf * HALF_TOKENS, (hf + 1) * HALF_TOKENS)
+            x_grouped = x_stage.tile([P, HALF_TOKENS, PACK], BF16, align_bytes=64)
             nc.scalar.copy(
                 out=x_grouped[:].bitcast(F32),
-                in_=xt_banks[b * PASSES + g][:].rearrange("q u w -> q w u"),
+                in_=xt_banks[hf * PASSES + g][:].rearrange("q u w -> q w u"),
             )
-            quantise(nc, x_codes[:, g, batch_cols], x_scales[:, g, batch_cols], x_grouped[:])
+            quantise(nc, x_codes[:, g, half_cols], x_scales[:, g, half_cols], x_grouped[:])
 
         wa_codes = keep.tile([P, PASSES, KVL], U32, align_bytes=64)
         wa_scales = keep.tile([P, PASSES, KVL], U8, align_bytes=64)
@@ -174,20 +190,23 @@ def tile_mlaattention_pb_kernel(tc, hidden_states, Wkva, Wkvb, k_full, v):
             quantise(nc, wa_codes[:, g, :], wa_scales[:, g, :], wa_grouped[:])
 
         ckv_acc = [
-            [banks.tile([P, S], F32, tag="bank", name="ckv_acc%d%d" % (b, m)) for m in range(PACK)]
-            for b in range(B)
+            [
+                banks.tile([P, HALF_TOKENS], F32, tag="bank", name="ckv_acc%d%d" % (hf, m))
+                for m in range(PACK)
+            ]
+            for hf in range(HALVES)
         ]
         for g in range(PASSES):
-            for b in range(B):
-                batch_cols = slice(b * S, (b + 1) * S)
+            for hf in range(HALVES):
+                half_cols = slice(hf * HALF_TOKENS, (hf + 1) * HALF_TOKENS)
                 for m in range(PACK):
                     latent = slice(m * P, (m + 1) * P)
                     nc.tensor.matmul_mx(
-                        out=ckv_acc[b][m][:],
+                        out=ckv_acc[hf][m][:],
                         lhsT=wa_codes[:, g, latent].bitcast(FP8X4),
                         lhsT_scale=wa_scales[:, g, latent],
-                        rhs=x_codes[:, g, batch_cols].bitcast(FP8X4),
-                        rhs_scale=x_scales[:, g, batch_cols],
+                        rhs=x_codes[:, g, half_cols].bitcast(FP8X4),
+                        rhs_scale=x_scales[:, g, half_cols],
                         start=(g == 0),
                         stop=(g == PASSES - 1),
                     )
@@ -215,13 +234,13 @@ def tile_mlaattention_pb_kernel(tc, hidden_states, Wkva, Wkvb, k_full, v):
         ckv_grouped = keep.tile([P, TOKENS, PACK], BF16, align_bytes=64)
         ckv_codes = keep.tile([P, TOKENS], U32, align_bytes=64)
         ckv_scales = keep.tile([P, TOKENS], U8, align_bytes=64)
-        for b in range(B):
-            batch_cols = slice(b * S, (b + 1) * S)
+        for hf in range(HALVES):
+            half_cols = slice(hf * HALF_TOKENS, (hf + 1) * HALF_TOKENS)
             for m in range(PACK):
-                nc.scalar.copy(out=ckv_rows[:, m, batch_cols], in_=ckv_acc[b][m][:])
-            regroup(nc.vector.tensor_copy, ckv_grouped[:, batch_cols, :], ckv_rows[:, :, batch_cols])
+                nc.scalar.copy(out=ckv_rows[:, m, half_cols], in_=ckv_acc[hf][m][:])
+            regroup(nc.vector.tensor_copy, ckv_grouped[:, half_cols, :], ckv_rows[:, :, half_cols])
             quantise(
-                nc, ckv_codes[:, batch_cols], ckv_scales[:, batch_cols], ckv_grouped[:, batch_cols, :]
+                nc, ckv_codes[:, half_cols], ckv_scales[:, half_cols], ckv_grouped[:, half_cols, :]
             )
 
         def second_matmul(out, c, weights):
@@ -242,18 +261,18 @@ def tile_mlaattention_pb_kernel(tc, hidden_states, Wkva, Wkvb, k_full, v):
             wv = wv_next
             if hg + 1 < GROUPS:
                 wv_next = quantised_weights(hg + 1, ND, VD)
-            v_out = outs.tile([P, B, GROUP_HEADS, POS_PER_PART, VD], F32)
+            v_out = outs.tile([P, GROUP_HEADS, CHUNKS, VD], F32)
+            for c in range(CHUNKS):
+                v_ps = banks.tile([P, GROUP_HEADS * VD], F32, tag="bank")
+                second_matmul(v_ps[:], c, wv)
+                nc.scalar.copy(
+                    out=v_out[:, :, c, :],
+                    in_=v_ps[:].rearrange("p (h d) -> p h d", h=GROUP_HEADS),
+                )
             for b in range(B):
-                for e in range(POS_PER_PART):
-                    v_ps = banks.tile([P, GROUP_HEADS * VD], F32, tag="bank")
-                    second_matmul(v_ps[:], b * POS_PER_PART + e, wv)
-                    nc.scalar.copy(
-                        out=v_out[:, b, :, e, :],
-                        in_=v_ps[:].rearrange("p (h d) -> p h d", h=GROUP_HEADS),
-                    )
                 nc.sync.dma_start(
-                    out=v[b, group_heads].rearrange("h (p e) d -> p h (e d)", e=POS_PER_PART),
-                    in_=v_out[:, b].rearrange("p h e d -> p h (e d)"),
+                    out=v[b, group_heads].rearrange("h (q c) d -> q h (c d)", c=CHUNKS),
+                    in_=v_out[b:P:B].rearrange("p h c d -> p h (c d)"),
                 )
 
         wr_codes = keep.tile([P, PASSES, RD], U32, align_bytes=64)
@@ -304,24 +323,24 @@ def tile_mlaattention_pb_kernel(tc, hidden_states, Wkva, Wkvb, k_full, v):
         for hg in range(GROUPS):
             group_heads = slice(hg * GROUP_HEADS, (hg + 1) * GROUP_HEADS)
             wk = wk_next
-            k_out = outs.tile([P, B, GROUP_HEADS, POS_PER_PART, HEAD_COLS], F32)
-            for b in range(B):
-                k_ps = banks.tile([P, POS_PER_PART, GROUP_HEADS * ND], F32, tag="bank")
-                for e in range(POS_PER_PART):
-                    second_matmul(k_ps[:, e, :], b * POS_PER_PART + e, wk)
+            k_out = outs.tile([P, GROUP_HEADS, CHUNKS, HEAD_COLS], F32)
+            nc.vector.tensor_copy(
+                out=k_out[:, :, :, ND:],
+                in_=kpe_rot[:].unsqueeze(1).to_broadcast([P, GROUP_HEADS, CHUNKS, RD]),
+            )
+            for hf in range(HALVES):
+                half_chunks = slice(hf * HALF_CHUNKS, (hf + 1) * HALF_CHUNKS)
+                k_ps = banks.tile([P, HALF_CHUNKS, GROUP_HEADS * ND], F32, tag="bank")
+                for e in range(HALF_CHUNKS):
+                    second_matmul(k_ps[:, e, :], hf * HALF_CHUNKS + e, wk)
                 nc.scalar.copy(
-                    out=k_out[:, b, :, :, 0:ND].rearrange("p h e d -> p e h d"),
+                    out=k_out[:, :, half_chunks, 0:ND].rearrange("p h e d -> p e h d"),
                     in_=k_ps[:].rearrange("p e (h d) -> p e h d", h=GROUP_HEADS),
                 )
-                nc.vector.tensor_copy(
-                    out=k_out[:, b, :, :, ND:],
-                    in_=kpe_rot[:, b * POS_PER_PART : (b + 1) * POS_PER_PART, :]
-                    .unsqueeze(1)
-                    .to_broadcast([P, GROUP_HEADS, POS_PER_PART, RD]),
-                )
+            for b in range(B):
                 nc.sync.dma_start(
-                    out=k_full[b, group_heads].rearrange("h (p e) d -> p h (e d)", e=POS_PER_PART),
-                    in_=k_out[:, b].rearrange("p h e d -> p h (e d)"),
+                    out=k_full[b, group_heads].rearrange("h (q c) d -> q h (c d)", c=CHUNKS),
+                    in_=k_out[b:P:B].rearrange("p h c d -> p h (c d)"),
                 )
             if hg + 1 < GROUPS:
                 wk_next = quantised_weights(hg + 1, 0, ND)

@@ -35,6 +35,7 @@ GROUP_COLS = GROUP_HEADS * HEAD_COLS
 HALF = RD // 2
 RUN = 4
 WA_VECTOR_COLS = 320
+KPE_GROUP = GROUPS - 2
 ROUND_MAGIC = 1.5 * 2.0**23
 
 FLOPS = 2 * TOKENS * D * WA_COLS + 2 * TOKENS * KVL * H * HEAD_COLS
@@ -66,11 +67,13 @@ def tile_mlaattention_pb_kernel(tc, hidden_states, Wkva, Wkvb, k_full, v):
         banks = stack.enter_context(tc.psum_pool(name="banks", bufs=8))
         stack.enter_context(tc.manual_schedule())
 
-        x_sb = keep.tile([P, HALVES, HALF_CHUNKS, D], BF16)
+        x_sb = [
+            keep.tile([P, HALF_CHUNKS, D], BF16, name="x_sb%d" % hf) for hf in range(HALVES)
+        ]
         for hf in range(HALVES):
             for b in range(B):
                 nc.sync.dma_start(
-                    out=x_sb[b:P:B, hf],
+                    out=x_sb[hf][b:P:B],
                     in_=hidden_states[b].rearrange(
                         "(q hf e) k -> hf q e k", hf=HALVES, e=HALF_CHUNKS
                     )[hf],
@@ -153,7 +156,7 @@ def tile_mlaattention_pb_kernel(tc, hidden_states, Wkva, Wkvb, k_full, v):
                         first = (2 * g + u) * P
                         nc.tensor.transpose(
                             out=xt[:, u, e * P : (e + 1) * P],
-                            in_=x_sb[:, hf, e, :].bitcast(F32)[:, first : first + P],
+                            in_=x_sb[hf][:, e, :].bitcast(F32)[:, first : first + P],
                             identity=ident[:],
                         )
                 xt_banks.append(xt)
@@ -256,9 +259,38 @@ def tile_mlaattention_pb_kernel(tc, hidden_states, Wkva, Wkvb, k_full, v):
                 stop=True,
             )
 
+        wr_codes = keep.tile([P, PASSES, RD], U32, align_bytes=64)
+        wr_scales = keep.tile([P, PASSES, RD], U8, align_bytes=64)
+        kpe_tiles = []
+
+        def quantise_rope_weights():
+            nc.vector.quantize_mx(
+                out=wr_codes[:].rearrange("p g c -> p (g c)").bitcast(FP8X4),
+                scales=wr_scales[:].rearrange("p g c -> p (g c)"),
+                in_=wr_grouped[:].rearrange("p g c t -> p (g c t)"),
+            )
+
+        def k_pe_passes():
+            kpe_ps = banks.tile([P, CHUNKS, RD], F32, tag="bank")
+            for c in range(CHUNKS):
+                tokens = slice(c * P, (c + 1) * P)
+                for g in range(PASSES):
+                    nc.tensor.matmul_mx(
+                        out=kpe_ps[:, c, :],
+                        lhsT=x_codes[:, g, tokens].bitcast(FP8X4),
+                        lhsT_scale=x_scales[:, g, tokens],
+                        rhs=wr_codes[:, g, :].bitcast(FP8X4),
+                        rhs_scale=wr_scales[:, g, :],
+                        start=(g == 0),
+                        stop=(g == PASSES - 1),
+                    )
+            kpe_tiles.append(kpe_ps)
+
         for hg in range(GROUPS):
             group_heads = slice(hg * GROUP_HEADS, (hg + 1) * GROUP_HEADS)
             wv = wv_next
+            if hg == KPE_GROUP:
+                quantise_rope_weights()
             if hg + 1 < GROUPS:
                 wv_next = quantised_weights(hg + 1, ND, VD)
             v_out = outs.tile([P, GROUP_HEADS, CHUNKS, VD], F32)
@@ -275,29 +307,12 @@ def tile_mlaattention_pb_kernel(tc, hidden_states, Wkva, Wkvb, k_full, v):
                     in_=v_out[b:P:B].rearrange("p h c d -> p h (c d)"),
                 )
 
-        wr_codes = keep.tile([P, PASSES, RD], U32, align_bytes=64)
-        wr_scales = keep.tile([P, PASSES, RD], U8, align_bytes=64)
-        nc.vector.quantize_mx(
-            out=wr_codes[:].rearrange("p g c -> p (g c)").bitcast(FP8X4),
-            scales=wr_scales[:].rearrange("p g c -> p (g c)"),
-            in_=wr_grouped[:].rearrange("p g c t -> p (g c t)"),
-        )
-        kpe_ps = banks.tile([P, CHUNKS, RD], F32, tag="bank")
-        for c in range(CHUNKS):
-            tokens = slice(c * P, (c + 1) * P)
-            for g in range(PASSES):
-                nc.tensor.matmul_mx(
-                    out=kpe_ps[:, c, :],
-                    lhsT=x_codes[:, g, tokens].bitcast(FP8X4),
-                    lhsT_scale=x_scales[:, g, tokens],
-                    rhs=wr_codes[:, g, :].bitcast(FP8X4),
-                    rhs_scale=wr_scales[:, g, :],
-                    start=(g == 0),
-                    stop=(g == PASSES - 1),
-                )
+            if hg == KPE_GROUP:
+                k_pe_passes()
+
         wk_next = quantised_weights(0, 0, ND)
 
-        kpe_pairs = kpe_ps[:].rearrange("p c (i j) -> p j c i", j=2)
+        kpe_pairs = kpe_tiles[0][:].rearrange("p c (i j) -> p j c i", j=2)
         table_shape = [P, 2, CHUNKS, HALF]
         by_cos = keep.tile(table_shape, F32)
         by_sin = keep.tile(table_shape, F32)

@@ -95,12 +95,15 @@ def tile_mlaattention_pb_kernel(tc, hidden_states, Wkva, Wkvb, k_full, v):
                 ),
             )
 
-        ident = keep.tile([P, P], F32)
-        make_identity(nc, ident[:])
         first_pos = keep.tile([P, 1], I32)
         nc.gpsimd.iota(first_pos[:], pattern=[[0, 1]], base=0, channel_multiplier=1)
         chunk_no = keep.tile([P, CHUNKS], I32)
         nc.gpsimd.iota(chunk_no[:], pattern=[[1, CHUNKS]], base=0, channel_multiplier=0)
+        ident = keep.tile([P, P], F32)
+        make_identity(nc, ident[:])
+        sin_warm = keep.tile([P, 1], F32)
+        nc.gpsimd.memset(sin_warm[:], 0.0)
+        nc.scalar.activation(out=sin_warm[:], in_=sin_warm[:], func=ACT.Sin)
         nc.vector.tensor_scalar(
             out=first_pos[:],
             in0=first_pos[:],
@@ -144,8 +147,6 @@ def tile_mlaattention_pb_kernel(tc, hidden_states, Wkva, Wkvb, k_full, v):
             op1=ALU.subtract,
         )
         nc.vector.tensor_tensor(out=whole[:], in0=turns[:], in1=whole[:], op=ALU.subtract)
-        cos_sin = keep.tile([P, 2, CHUNKS, HALF], F32)
-        nc.scalar.activation(out=cos_sin[:], in_=whole[:], func=ACT.Sin, scale=2.0 * math.pi)
 
         xt_banks = []
         for hf in range(HALVES):
@@ -218,6 +219,8 @@ def tile_mlaattention_pb_kernel(tc, hidden_states, Wkva, Wkvb, k_full, v):
         for g in range(PASSES):
             wa_rows = wa_raw[:, g].rearrange("p u (e c) -> p (u e) c", e=2)
             regroup(nc.scalar.copy, wr_grouped[:, g], wa_rows[:, :, KVL:])
+        cos_sin = keep.tile([P, 2, CHUNKS, HALF], F32)
+        nc.scalar.activation(out=cos_sin[:], in_=whole[:], func=ACT.Sin, scale=2.0 * math.pi)
 
         def quantised_weights(hg, first, size):
             heads = wb_raw[:, hg].rearrange("p t (h d) -> p t h d", h=GROUP_HEADS)

@@ -33,7 +33,7 @@ GROUP_HEADS = 4
 GROUPS = H // GROUP_HEADS
 GROUP_COLS = GROUP_HEADS * HEAD_COLS
 HALF = RD // 2
-RUN = 4
+RUN = 8
 WA_VECTOR_COLS = 320
 KPE_GROUP = GROUPS - 2
 ROUND_MAGIC = 1.5 * 2.0**23

@@ -31,11 +31,13 @@ WA_COLS = KVL + RD
 HEAD_COLS = ND + VD
 GROUP_HEADS = 4
 GROUPS = H // GROUP_HEADS
+STEPS = (("v", 0, 4), ("v", 4, 2), ("v", 6, 2), ("k", 0, 4), ("k", 4, 4), ("v", 8, 4), ("k", 8, 4), ("v", 12, 4), ("k", 12, 4))
+K_HEADS = 2
+K_BUFS = 4
 GROUP_COLS = GROUP_HEADS * HEAD_COLS
 HALF = RD // 2
 RUN = 8
 WA_VECTOR_COLS = 320
-KPE_GROUP = GROUPS - 2
 ROUND_MAGIC = 1.5 * 2.0**23
 
 FLOPS = 2 * TOKENS * D * WA_COLS + 2 * TOKENS * KVL * H * HEAD_COLS
@@ -60,23 +62,19 @@ def tile_mlaattention_pb_kernel(tc, hidden_states, Wkva, Wkvb, k_full, v):
     nc = tc.nc
     with ExitStack() as stack:
         keep = stack.enter_context(tc.tile_pool(name="keep", bufs=1))
-        stage = stack.enter_context(tc.tile_pool(name="stage", bufs=2))
+        stage = stack.enter_context(tc.tile_pool(name="stage", bufs=3))
         x_stage = stack.enter_context(tc.tile_pool(name="x_stage", bufs=4))
-        per_group = stack.enter_context(tc.tile_pool(name="per_group", bufs=GROUPS))
+        per_group = stack.enter_context(tc.tile_pool(name="per_group", bufs=4))
         outs = stack.enter_context(tc.tile_pool(name="outs", bufs=3))
         banks = stack.enter_context(tc.psum_pool(name="banks", bufs=8))
         stack.enter_context(tc.manual_schedule())
 
-        x_sb = [
-            keep.tile([P, HALF_CHUNKS, D], BF16, name="x_sb%d" % hf) for hf in range(HALVES)
-        ]
-        for hf in range(HALVES):
+        x_sb = [keep.tile([P, D], BF16, name="x_sb%d" % c) for c in range(CHUNKS)]
+        for c in range(CHUNKS):
             for b in range(B):
                 nc.sync.dma_start(
-                    out=x_sb[hf][b:P:B],
-                    in_=hidden_states[b].rearrange(
-                        "(q hf e) k -> hf q e k", hf=HALVES, e=HALF_CHUNKS
-                    )[hf],
+                    out=x_sb[c][b:P:B],
+                    in_=hidden_states[b].rearrange("(q c) k -> c q k", c=CHUNKS)[c],
                 )
         wa_raw = keep.tile([P, PASSES, 2, 2 * WA_COLS], BF16)
         for g in range(PASSES):
@@ -147,50 +145,110 @@ def tile_mlaattention_pb_kernel(tc, hidden_states, Wkva, Wkvb, k_full, v):
             op1=ALU.subtract,
         )
         nc.vector.tensor_tensor(out=whole[:], in0=turns[:], in1=whole[:], op=ALU.subtract)
+        cos_sin = keep.tile([P, 2, CHUNKS, HALF, 2], F32)
+
+        def sines():
+            two_pi = 2.0 * math.pi
+            nc.scalar.activation(
+                out=cos_sin[:, 0],
+                in_=whole[:, 0].unsqueeze(3).to_broadcast([P, CHUNKS, HALF, 2]),
+                func=ACT.Sin,
+                scale=two_pi,
+            )
+            for j, sign in enumerate((-1.0, 1.0)):
+                nc.scalar.activation(
+                    out=cos_sin[:, 1, :, :, j], in_=whole[:, 1], func=ACT.Sin, scale=sign * two_pi
+                )
 
         xt_banks = []
         for hf in range(HALVES):
-            for g in range(PASSES):
-                xt = banks.tile([P, 2, HALF_TOKENS], F32, tag="bank")
-                for u in range(2):
-                    for e in range(HALF_CHUNKS):
+            half_banks = [
+                banks.tile([P, 2, HALF_TOKENS], F32, tag="bank", name="xt%d%d" % (hf, g))
+                for g in range(PASSES)
+            ]
+            for e in range(HALF_CHUNKS):
+                for g in range(PASSES):
+                    for u in range(2):
                         first = (2 * g + u) * P
                         nc.tensor.transpose(
-                            out=xt[:, u, e * P : (e + 1) * P],
-                            in_=x_sb[hf][:, e, :].bitcast(F32)[:, first : first + P],
+                            out=half_banks[g][:, u, e * P : (e + 1) * P],
+                            in_=x_sb[hf * HALF_CHUNKS + e][:].bitcast(F32)[:, first : first + P],
                             identity=ident[:],
                         )
-                xt_banks.append(xt)
-        x_codes = keep.tile([P, PASSES, TOKENS], U32, align_bytes=64)
-        x_scales = keep.tile([P, PASSES, TOKENS], U8, align_bytes=64)
+            xt_banks.extend(half_banks)
+        x_codes = keep.tile([P, HALVES, PASSES, HALF_TOKENS], U32, align_bytes=64)
+        x_scales = keep.tile([P, HALVES, PASSES, HALF_TOKENS], U8, align_bytes=64)
 
-        def quantise_x(hf, g):
-            half_cols = slice(hf * HALF_TOKENS, (hf + 1) * HALF_TOKENS)
-            x_grouped = x_stage.tile([P, HALF_TOKENS, PACK], BF16, align_bytes=64)
-            nc.scalar.copy(
-                out=x_grouped[:].bitcast(F32),
+        def x_pair():
+            x_grouped = x_stage.tile([P, 2, HALF_TOKENS, PACK], BF16, align_bytes=64)
+            return x_grouped
+
+        def copy_x(copy, hf, g, x_grouped):
+            copy(
+                out=x_grouped[:, g % 2]
+                .rearrange("q w t -> q (w t)")
+                .bitcast(F32)
+                .rearrange("q (w u) -> q w u", u=2),
                 in_=xt_banks[hf * PASSES + g][:].rearrange("q u w -> q w u"),
             )
-            quantise(nc, x_codes[:, g, half_cols], x_scales[:, g, half_cols], x_grouped[:])
+
+        def quantise_x(hf, g, x_grouped):
+            quantise(
+                nc,
+                x_codes[:, hf, g : g + 2].rearrange("p g w -> p (g w)"),
+                x_scales[:, hf, g : g + 2].rearrange("p g w -> p (g w)"),
+                x_grouped[:].rearrange("p g w t -> p (g w) t"),
+            )
 
         wa_codes = keep.tile([P, PASSES, KVL], U32, align_bytes=64)
         wa_scales = keep.tile([P, PASSES, KVL], U8, align_bytes=64)
-        for g in range(PASSES):
-            quantise_x(0, g)
-        for g in range(PASSES):
-            quantise_x(1, g)
-            wa_rows = wa_raw[:, g].rearrange("p u (e c) -> p (u e) c", e=2)
+        wr_grouped = keep.tile([P, PASSES, RD, PACK], BF16, align_bytes=64)
+        wr_codes = keep.tile([P, PASSES, RD], U32, align_bytes=64)
+        wr_scales = keep.tile([P, PASSES, RD], U8, align_bytes=64)
+
+        def wa_rows(g):
+            return wa_raw[:, g].rearrange("p u (e c) -> p (u e) c", e=2)
+
+        def regroup_wa(g):
             wa_grouped = stage.tile([P, KVL, PACK], BF16, align_bytes=64)
             regroup(
                 nc.vector.tensor_copy,
                 wa_grouped[:, 0:WA_VECTOR_COLS, :],
-                wa_rows[:, :, 0:WA_VECTOR_COLS],
+                wa_rows(g)[:, :, 0:WA_VECTOR_COLS],
             )
             regroup(
                 nc.scalar.copy,
                 wa_grouped[:, WA_VECTOR_COLS:, :],
-                wa_rows[:, :, WA_VECTOR_COLS:KVL],
+                wa_rows(g)[:, :, WA_VECTOR_COLS:KVL],
             )
+            return wa_grouped
+
+        def regroup_wr(copy, g):
+            regroup(copy, wr_grouped[:, g], wa_rows(g)[:, :, KVL:])
+
+        def quantise_rope_weights():
+            quantise(
+                nc,
+                wr_codes[:].rearrange("p g c -> p (g c)"),
+                wr_scales[:].rearrange("p g c -> p (g c)"),
+                wr_grouped[:].rearrange("p g c t -> p (g c) t"),
+            )
+
+        for g in range(0, PASSES, 2):
+            x_now = x_pair()
+            copy_x(nc.scalar.copy, 0, g, x_now)
+            copy_x(nc.vector.tensor_copy if g + 1 in (1,) else nc.scalar.copy, 0, g + 1, x_now)
+            quantise_x(0, g, x_now)
+        x_now = x_pair()
+        copy_x(nc.scalar.copy, 1, 0, x_now)
+        for g in range(PASSES):
+            wa_grouped = regroup_wa(g)
+            if g + 1 < PASSES:
+                x_next = x_now if g % 2 == 0 else x_pair()
+                copy_x(nc.scalar.copy, 1, g + 1, x_next)
+            if g % 2 == 1:
+                quantise_x(1, g - 1, x_now)
+            x_now = x_next
             quantise(nc, wa_codes[:, g, :], wa_scales[:, g, :], wa_grouped[:])
 
         ckv_acc = [
@@ -202,52 +260,78 @@ def tile_mlaattention_pb_kernel(tc, hidden_states, Wkva, Wkvb, k_full, v):
         ]
         for g in range(PASSES):
             for hf in range(HALVES):
-                half_cols = slice(hf * HALF_TOKENS, (hf + 1) * HALF_TOKENS)
                 for m in range(PACK):
                     latent = slice(m * P, (m + 1) * P)
                     nc.tensor.matmul_mx(
                         out=ckv_acc[hf][m][:],
                         lhsT=wa_codes[:, g, latent].bitcast(FP8X4),
                         lhsT_scale=wa_scales[:, g, latent],
-                        rhs=x_codes[:, g, half_cols].bitcast(FP8X4),
-                        rhs_scale=x_scales[:, g, half_cols],
+                        rhs=x_codes[:, hf, g, :].bitcast(FP8X4),
+                        rhs_scale=x_scales[:, hf, g, :],
                         start=(g == 0),
                         stop=(g == PASSES - 1),
                     )
 
-        wr_grouped = keep.tile([P, PASSES, RD, PACK], BF16, align_bytes=64)
-        for g in range(PASSES):
-            wa_rows = wa_raw[:, g].rearrange("p u (e c) -> p (u e) c", e=2)
-            regroup(nc.scalar.copy, wr_grouped[:, g], wa_rows[:, :, KVL:])
-        cos_sin = keep.tile([P, 2, CHUNKS, HALF], F32)
-        nc.scalar.activation(out=cos_sin[:], in_=whole[:], func=ACT.Sin, scale=2.0 * math.pi)
+        def regroup_weights(h0, heads, first, size, scalar_heads=0):
+            h1 = h0 % GROUP_HEADS
+            split = heads - scalar_heads
+            words = heads * size
+            grouped = stage.tile([P, words, PACK], BF16, align_bytes=64, tag="wb%d" % words)
+            by_head = grouped[:].rearrange("p (h c i) t -> p h c t i", h=heads, i=RUN)
+            from_head = wb_raw[:, h0 // GROUP_HEADS].rearrange("p t (h d) -> p t h d", h=GROUP_HEADS)[
+                :, :, h1 : h1 + heads, first : first + size
+            ].rearrange("p t h (c i) -> p h c t i", i=RUN)
+            nc.vector.tensor_copy(out=by_head[:, :split], in_=from_head[:, :split])
+            if scalar_heads:
+                nc.scalar.copy(out=by_head[:, split:], in_=from_head[:, split:])
+            return grouped
 
-        def quantised_weights(hg, first, size):
-            heads = wb_raw[:, hg].rearrange("p t (h d) -> p t h d", h=GROUP_HEADS)
-            grouped = stage.tile([P, GROUP_HEADS * size, PACK], BF16, align_bytes=64, tag="wb%d" % size)
-            nc.vector.tensor_copy(
-                out=grouped[:].rearrange("p (h c i) t -> p h c t i", h=GROUP_HEADS, i=RUN),
-                in_=heads[:, :, :, first : first + size].rearrange("p t h (c i) -> p h c t i", i=RUN),
-            )
-            codes = per_group.tile([P, GROUP_HEADS * size], U32, align_bytes=64, tag="codes%d" % size)
-            scales = per_group.tile([P, GROUP_HEADS * size], U8, align_bytes=64, tag="scales%d" % size)
+        def quantise_weights(grouped):
+            words = grouped.shape[1]
+            codes = per_group.tile([P, words], U32, align_bytes=64, tag="codes%d" % words)
+            scales = per_group.tile([P, words], U8, align_bytes=64, tag="scales%d" % words)
             quantise(nc, codes[:], scales[:], grouped[:])
             return codes, scales
-
-        wv_next = quantised_weights(0, ND, VD)
 
         ckv_rows = keep.tile([P, PACK, TOKENS], BF16)
         ckv_grouped = keep.tile([P, TOKENS, PACK], BF16, align_bytes=64)
         ckv_codes = keep.tile([P, TOKENS], U32, align_bytes=64)
         ckv_scales = keep.tile([P, TOKENS], U8, align_bytes=64)
-        for hf in range(HALVES):
-            half_cols = slice(hf * HALF_TOKENS, (hf + 1) * HALF_TOKENS)
-            for m in range(PACK):
-                nc.scalar.copy(out=ckv_rows[:, m, half_cols], in_=ckv_acc[hf][m][:])
-            regroup(nc.vector.tensor_copy, ckv_grouped[:, half_cols, :], ckv_rows[:, :, half_cols])
+
+        def half_of(hf):
+            return slice(hf * HALF_TOKENS, (hf + 1) * HALF_TOKENS)
+
+        def copy_ckv(copy, hf, m):
+            copy(out=ckv_rows[:, m, half_of(hf)], in_=ckv_acc[hf][m][:])
+
+        def regroup_ckv(hf):
+            regroup(nc.vector.tensor_copy, ckv_grouped[:, half_of(hf), :], ckv_rows[:, :, half_of(hf)])
+
+        def quantise_ckv(hf):
             quantise(
-                nc, ckv_codes[:, half_cols], ckv_scales[:, half_cols], ckv_grouped[:, half_cols, :]
+                nc, ckv_codes[:, half_of(hf)], ckv_scales[:, half_of(hf)], ckv_grouped[:, half_of(hf), :]
             )
+
+        regroup_wr(nc.scalar.copy, 0)
+        regroup_wr(nc.scalar.copy, 1)
+        regroup_wr(nc.scalar.copy, 2)
+        regroup_wr(nc.scalar.copy, 3)
+        first_values = regroup_weights(0, STEPS[0][2], ND, VD, 0)
+        weights = quantise_weights(first_values)
+        quantise_rope_weights()
+        copy_ckv(nc.scalar.copy, 0, 0)
+        copy_ckv(nc.scalar.copy, 0, 1)
+        copy_ckv(nc.scalar.copy, 0, 2)
+        copy_ckv(nc.scalar.copy, 0, 3)
+        regroup_ckv(0)
+        quantise_ckv(0)
+        copy_ckv(nc.scalar.copy, 1, 0)
+        copy_ckv(nc.scalar.copy, 1, 1)
+        copy_ckv(nc.scalar.copy, 1, 2)
+        copy_ckv(nc.scalar.copy, 1, 3)
+        sines()
+        regroup_ckv(1)
+        quantise_ckv(1)
 
         def second_matmul(out, c, weights):
             codes, scales = weights
@@ -262,103 +346,114 @@ def tile_mlaattention_pb_kernel(tc, hidden_states, Wkva, Wkvb, k_full, v):
                 stop=True,
             )
 
-        wr_codes = keep.tile([P, PASSES, RD], U32, align_bytes=64)
-        wr_scales = keep.tile([P, PASSES, RD], U8, align_bytes=64)
-        kpe_tiles = []
+        def k_pe_passes(kpe_ps, c):
+            hf, e = divmod(c, HALF_CHUNKS)
+            tokens = slice(e * P, (e + 1) * P)
+            for g in range(PASSES):
+                nc.tensor.matmul_mx(
+                    out=kpe_ps[:, c, :],
+                    lhsT=x_codes[:, hf, g, tokens].bitcast(FP8X4),
+                    lhsT_scale=x_scales[:, hf, g, tokens],
+                    rhs=wr_codes[:, g, :].bitcast(FP8X4),
+                    rhs_scale=wr_scales[:, g, :],
+                    start=(g == 0),
+                    stop=(g == PASSES - 1),
+                )
 
-        def quantise_rope_weights():
-            nc.vector.quantize_mx(
-                out=wr_codes[:].rearrange("p g c -> p (g c)").bitcast(FP8X4),
-                scales=wr_scales[:].rearrange("p g c -> p (g c)"),
-                in_=wr_grouped[:].rearrange("p g c t -> p (g c t)"),
+        pairs_shape = [P, CHUNKS, HALF, 2]
+        by_cos = keep.tile(pairs_shape, F32)
+        by_sin = keep.tile(pairs_shape, F32)
+        kpe_rot = keep.tile([P, CHUNKS, RD], F32)
+
+        def rotate(kpe_ps):
+            pairs = kpe_ps[:].rearrange("p c (i j) -> p c i j", j=2)
+            nc.vector.tensor_tensor(out=by_cos[:], in0=pairs, in1=cos_sin[:, 0], op=ALU.mult)
+            nc.vector.tensor_tensor(
+                out=by_sin[:], in0=pairs[:, :, :, ::-1], in1=cos_sin[:, 1], op=ALU.mult
+            )
+            nc.vector.tensor_tensor(
+                out=kpe_rot[:].rearrange("p c (i j) -> p c i j", j=2),
+                in0=by_cos[:],
+                in1=by_sin[:],
+                op=ALU.add,
             )
 
-        def k_pe_passes():
-            kpe_ps = banks.tile([P, CHUNKS, RD], F32, tag="bank")
-            for c in range(CHUNKS):
-                tokens = slice(c * P, (c + 1) * P)
-                for g in range(PASSES):
-                    nc.tensor.matmul_mx(
-                        out=kpe_ps[:, c, :],
-                        lhsT=x_codes[:, g, tokens].bitcast(FP8X4),
-                        lhsT_scale=x_scales[:, g, tokens],
-                        rhs=wr_codes[:, g, :].bitcast(FP8X4),
-                        rhs_scale=wr_scales[:, g, :],
-                        start=(g == 0),
-                        stop=(g == PASSES - 1),
-                    )
-            kpe_tiles.append(kpe_ps)
+        k_rows = [
+            keep.tile([P, K_HEADS, CHUNKS, HEAD_COLS], F32, name="k_rows%d" % i)
+            for i in range(K_BUFS)
+        ]
 
-        for hg in range(GROUPS):
-            group_heads = slice(hg * GROUP_HEADS, (hg + 1) * GROUP_HEADS)
-            wv = wv_next
-            if hg == KPE_GROUP:
-                quantise_rope_weights()
-            if hg + 1 < GROUPS:
-                wv_next = quantised_weights(hg + 1, ND, VD)
-            v_out = outs.tile([P, GROUP_HEADS, CHUNKS, VD], F32)
-            for c in range(CHUNKS):
-                v_ps = banks.tile([P, GROUP_HEADS * VD], F32, tag="bank")
-                second_matmul(v_ps[:], c, wv)
+        def lay_k_pe(copy, i):
+            copy(
+                out=k_rows[i][:, :, :, ND:],
+                in_=kpe_rot[:].unsqueeze(1).to_broadcast([P, K_HEADS, CHUNKS, RD]),
+            )
+
+        def key_matmuls(weights):
+            k_ps = []
+            for hf in range(HALVES):
+                ps = banks.tile([P, HALF_CHUNKS, GROUP_HEADS * ND], F32, tag="bank")
+                for e in range(HALF_CHUNKS):
+                    second_matmul(ps[:, e, :], hf * HALF_CHUNKS + e, weights)
+                k_ps.append(ps)
+            return k_ps
+
+        def key_rows(h0, k_ps):
+            k_out = k_rows[h0 // K_HEADS % K_BUFS]
+            h1 = h0 % GROUP_HEADS
+            for hf in range(HALVES):
+                half_chunks = slice(hf * HALF_CHUNKS, (hf + 1) * HALF_CHUNKS)
                 nc.scalar.copy(
-                    out=v_out[:, :, c, :],
-                    in_=v_ps[:].rearrange("p (h d) -> p h d", h=GROUP_HEADS),
+                    out=k_out[:, :, half_chunks, 0:ND].rearrange("p h e d -> p e h d"),
+                    in_=k_ps[hf][:].rearrange("p e (h d) -> p e h d", h=GROUP_HEADS)[
+                        :, :, h1 : h1 + K_HEADS
+                    ],
                 )
             for b in range(B):
                 nc.sync.dma_start(
-                    out=v[b, group_heads].rearrange("h (q c) d -> q h (c d)", c=CHUNKS),
+                    out=k_full[b, h0 : h0 + K_HEADS].rearrange("h (q c) d -> q h (c d)", c=CHUNKS),
+                    in_=k_out[b:P:B].rearrange("p h c d -> p h (c d)"),
+                )
+
+        def value_group(h0, heads, weights, last_copy):
+            v_out = outs.tile([P, heads, CHUNKS, VD], F32, tag="v_out%d" % heads)
+            per_bank = GROUP_HEADS // heads
+            for c in range(0, CHUNKS, per_bank):
+                v_ps = banks.tile([P, per_bank, heads * VD], F32, tag="bank")
+                for e in range(per_bank):
+                    second_matmul(v_ps[:, e, :], c + e, weights)
+                copy = last_copy if c + per_bank == CHUNKS else nc.scalar.copy
+                copy(
+                    out=v_out[:, :, c : c + per_bank, :].rearrange("p h e d -> p e h d"),
+                    in_=v_ps[:].rearrange("p e (h d) -> p e h d", h=heads),
+                )
+            for b in range(B):
+                nc.sync.dma_start(
+                    out=v[b, h0 : h0 + heads].rearrange("h (q c) d -> q h (c d)", c=CHUNKS),
                     in_=v_out[b:P:B].rearrange("p h c d -> p h (c d)"),
                 )
 
-            if hg == KPE_GROUP:
-                k_pe_passes()
-
-        wk_next = quantised_weights(0, 0, ND)
-
-        kpe_pairs = kpe_tiles[0][:].rearrange("p c (i j) -> p j c i", j=2)
-        table_shape = [P, 2, CHUNKS, HALF]
-        by_cos = keep.tile(table_shape, F32)
-        by_sin = keep.tile(table_shape, F32)
-        nc.vector.tensor_tensor(
-            out=by_cos[:],
-            in0=kpe_pairs,
-            in1=cos_sin[:, 0].unsqueeze(1).to_broadcast(table_shape),
-            op=ALU.mult,
-        )
-        nc.vector.tensor_tensor(
-            out=by_sin[:],
-            in0=kpe_pairs,
-            in1=cos_sin[:, 1].unsqueeze(1).to_broadcast(table_shape),
-            op=ALU.mult,
-        )
-        kpe_rot = keep.tile([P, CHUNKS, RD], F32)
-        rot_pairs = kpe_rot[:].rearrange("p c (i j) -> p j c i", j=2)
-        nc.vector.tensor_tensor(
-            out=rot_pairs[:, 0], in0=by_cos[:, 0], in1=by_sin[:, 1], op=ALU.subtract
-        )
-        nc.vector.tensor_tensor(out=rot_pairs[:, 1], in0=by_cos[:, 1], in1=by_sin[:, 0], op=ALU.add)
-
-        for hg in range(GROUPS):
-            group_heads = slice(hg * GROUP_HEADS, (hg + 1) * GROUP_HEADS)
-            wk = wk_next
-            k_out = outs.tile([P, GROUP_HEADS, CHUNKS, HEAD_COLS], F32)
-            nc.vector.tensor_copy(
-                out=k_out[:, :, :, ND:],
-                in_=kpe_rot[:].unsqueeze(1).to_broadcast([P, GROUP_HEADS, CHUNKS, RD]),
-            )
-            for hf in range(HALVES):
-                half_chunks = slice(hf * HALF_CHUNKS, (hf + 1) * HALF_CHUNKS)
-                k_ps = banks.tile([P, HALF_CHUNKS, GROUP_HEADS * ND], F32, tag="bank")
-                for e in range(HALF_CHUNKS):
-                    second_matmul(k_ps[:, e, :], hf * HALF_CHUNKS + e, wk)
-                nc.scalar.copy(
-                    out=k_out[:, :, half_chunks, 0:ND].rearrange("p h e d -> p e h d"),
-                    in_=k_ps[:].rearrange("p e (h d) -> p e h d", h=GROUP_HEADS),
-                )
-            for b in range(B):
-                nc.sync.dma_start(
-                    out=k_full[b, group_heads].rearrange("h (q c) d -> q h (c d)", c=CHUNKS),
-                    in_=k_out[b:P:B].rearrange("p h c d -> p h (c d)"),
-                )
-            if hg + 1 < GROUPS:
-                wk_next = quantised_weights(hg + 1, 0, ND)
+        kpe_ps = banks.tile([P, CHUNKS, RD], F32, tag="bank")
+        for n, (kind, h0, heads) in enumerate(STEPS):
+            now = weights
+            if n + 1 < len(STEPS):
+                next_kind, next_h0, next_heads = STEPS[n + 1]
+                if next_kind == "v":
+                    weights = quantise_weights(regroup_weights(next_h0, next_heads, ND, VD, 2 if next_heads == GROUP_HEADS else 0))
+                else:
+                    weights = quantise_weights(regroup_weights(next_h0, next_heads, 0, ND))
+                if next_kind == "k" and next_h0 == 0:
+                    rotate(kpe_ps)
+                    lay_k_pe(nc.vector.tensor_copy, 0)
+                    lay_k_pe(nc.vector.tensor_copy, 1)
+            if kind == "v":
+                value_group(h0, heads, now, nc.scalar.copy)
+            else:
+                k_ps = key_matmuls(now)
+                for h in range(h0, h0 + GROUP_HEADS, K_HEADS):
+                    if K_HEADS * 2 <= h < K_HEADS * K_BUFS:
+                        lay_k_pe(nc.vector.tensor_copy, h // K_HEADS)
+                    key_rows(h, k_ps)
+            if n == 0:
+                for c in (0, 1, 2, 3):
+                    k_pe_passes(kpe_ps, c)

@@ -37,7 +37,6 @@ K_BUFS = 4
 GROUP_COLS = GROUP_HEADS * HEAD_COLS
 HALF = RD // 2
 RUN = 8
-WA_VECTOR_COLS = 320
 ROUND_MAGIC = 1.5 * 2.0**23
 
 FLOPS = 2 * TOKENS * D * WA_COLS + 2 * TOKENS * KVL * H * HEAD_COLS
@@ -70,20 +69,30 @@ def tile_mlaattention_pb_kernel(tc, hidden_states, Wkva, Wkvb, k_full, v):
         stack.enter_context(tc.manual_schedule())
 
         x_sb = [keep.tile([P, D], BF16, name="x_sb%d" % c) for c in range(CHUNKS)]
-        for c in range(CHUNKS):
-            for b in range(B):
-                nc.sync.dma_start(
-                    out=x_sb[c][b:P:B],
-                    in_=hidden_states[b].rearrange("(q c) k -> c q k", c=CHUNKS)[c],
-                )
         wa_raw = keep.tile([P, PASSES, 2, 2 * WA_COLS], BF16)
-        for g in range(PASSES):
+
+        def load_x(hf):
+            for c in range(hf * HALF_CHUNKS, (hf + 1) * HALF_CHUNKS):
+                for b in range(B):
+                    nc.sync.dma_start(
+                        out=x_sb[c][b:P:B],
+                        in_=hidden_states[b].rearrange("(q c) k -> c q k", c=CHUNKS)[c],
+                    )
+
+        def load_wa(g):
             nc.sync.dma_start(
                 out=wa_raw[:, g],
                 in_=Wkva[g * K_PASS : (g + 1) * K_PASS, :].rearrange(
                     "(u q e) c -> q u (e c)", u=2, e=2
                 ),
             )
+
+        load_x(0)
+        load_wa(0)
+        load_x(1)
+        load_wa(1)
+        load_wa(2)
+        load_wa(3)
         wb_raw = keep.tile([P, GROUPS, PACK, GROUP_COLS], BF16)
         for hg in range(GROUPS):
             nc.sync.dma_start(
@@ -160,22 +169,21 @@ def tile_mlaattention_pb_kernel(tc, hidden_states, Wkva, Wkvb, k_full, v):
                     out=cos_sin[:, 1, :, :, j], in_=whole[:, 1], func=ACT.Sin, scale=sign * two_pi
                 )
 
-        xt_banks = []
-        for hf in range(HALVES):
-            half_banks = [
-                banks.tile([P, 2, HALF_TOKENS], F32, tag="bank", name="xt%d%d" % (hf, g))
-                for g in range(PASSES)
-            ]
+        xt_banks = {}
+
+        def transposes(hf):
+            for g in range(PASSES):
+                xt_banks[hf, g] = banks.tile([P, 2, HALF_TOKENS], F32, tag="bank", name="xt%d%d" % (hf, g))
             for e in range(HALF_CHUNKS):
                 for g in range(PASSES):
                     for u in range(2):
                         first = (2 * g + u) * P
                         nc.tensor.transpose(
-                            out=half_banks[g][:, u, e * P : (e + 1) * P],
+                            out=xt_banks[hf, g][:, u, e * P : (e + 1) * P],
                             in_=x_sb[hf * HALF_CHUNKS + e][:].bitcast(F32)[:, first : first + P],
                             identity=ident[:],
                         )
-            xt_banks.extend(half_banks)
+
         x_codes = keep.tile([P, HALVES, PASSES, HALF_TOKENS], U32, align_bytes=64)
         x_scales = keep.tile([P, HALVES, PASSES, HALF_TOKENS], U8, align_bytes=64)
 
@@ -189,7 +197,7 @@ def tile_mlaattention_pb_kernel(tc, hidden_states, Wkva, Wkvb, k_full, v):
                 .rearrange("q w t -> q (w t)")
                 .bitcast(F32)
                 .rearrange("q (w u) -> q w u", u=2),
-                in_=xt_banks[hf * PASSES + g][:].rearrange("q u w -> q w u"),
+                in_=xt_banks[hf, g][:].rearrange("q u w -> q w u"),
             )
 
         def quantise_x(hf, g, x_grouped):
@@ -209,17 +217,17 @@ def tile_mlaattention_pb_kernel(tc, hidden_states, Wkva, Wkvb, k_full, v):
         def wa_rows(g):
             return wa_raw[:, g].rearrange("p u (e c) -> p (u e) c", e=2)
 
-        def regroup_wa(g):
+        def regroup_wa(g, vector_cols):
             wa_grouped = stage.tile([P, KVL, PACK], BF16, align_bytes=64)
             regroup(
                 nc.vector.tensor_copy,
-                wa_grouped[:, 0:WA_VECTOR_COLS, :],
-                wa_rows(g)[:, :, 0:WA_VECTOR_COLS],
+                wa_grouped[:, 0:vector_cols, :],
+                wa_rows(g)[:, :, 0:vector_cols],
             )
             regroup(
                 nc.scalar.copy,
-                wa_grouped[:, WA_VECTOR_COLS:, :],
-                wa_rows(g)[:, :, WA_VECTOR_COLS:KVL],
+                wa_grouped[:, vector_cols:, :],
+                wa_rows(g)[:, :, vector_cols:KVL],
             )
             return wa_grouped
 
@@ -234,43 +242,25 @@ def tile_mlaattention_pb_kernel(tc, hidden_states, Wkva, Wkvb, k_full, v):
                 wr_grouped[:].rearrange("p g c t -> p (g c) t"),
             )
 
-        for g in range(0, PASSES, 2):
-            x_now = x_pair()
-            copy_x(nc.scalar.copy, 0, g, x_now)
-            copy_x(nc.vector.tensor_copy if g + 1 in (1,) else nc.scalar.copy, 0, g + 1, x_now)
-            quantise_x(0, g, x_now)
-        x_now = x_pair()
-        copy_x(nc.scalar.copy, 1, 0, x_now)
-        for g in range(PASSES):
-            wa_grouped = regroup_wa(g)
-            if g + 1 < PASSES:
-                x_next = x_now if g % 2 == 0 else x_pair()
-                copy_x(nc.scalar.copy, 1, g + 1, x_next)
-            if g % 2 == 1:
-                quantise_x(1, g - 1, x_now)
-            x_now = x_next
+        def quantise_wa(g, wa_grouped):
             quantise(nc, wa_codes[:, g, :], wa_scales[:, g, :], wa_grouped[:])
 
-        ckv_acc = [
-            [
-                banks.tile([P, HALF_TOKENS], F32, tag="bank", name="ckv_acc%d%d" % (hf, m))
-                for m in range(PACK)
-            ]
-            for hf in range(HALVES)
-        ]
-        for g in range(PASSES):
-            for hf in range(HALVES):
-                for m in range(PACK):
-                    latent = slice(m * P, (m + 1) * P)
-                    nc.tensor.matmul_mx(
-                        out=ckv_acc[hf][m][:],
-                        lhsT=wa_codes[:, g, latent].bitcast(FP8X4),
-                        lhsT_scale=wa_scales[:, g, latent],
-                        rhs=x_codes[:, hf, g, :].bitcast(FP8X4),
-                        rhs_scale=x_scales[:, hf, g, :],
-                        start=(g == 0),
-                        stop=(g == PASSES - 1),
-                    )
+        ckv_acc = {}
+
+        def first_matmul(hf, g):
+            for m in range(PACK):
+                if g == 0:
+                    ckv_acc[hf, m] = banks.tile([P, HALF_TOKENS], F32, tag="bank", name="ckv_acc%d%d" % (hf, m))
+                latent = slice(m * P, (m + 1) * P)
+                nc.tensor.matmul_mx(
+                    out=ckv_acc[hf, m][:],
+                    lhsT=wa_codes[:, g, latent].bitcast(FP8X4),
+                    lhsT_scale=wa_scales[:, g, latent],
+                    rhs=x_codes[:, hf, g, :].bitcast(FP8X4),
+                    rhs_scale=x_scales[:, hf, g, :],
+                    start=(g == 0),
+                    stop=(g == PASSES - 1),
+                )
 
         def regroup_weights(h0, heads, first, size, scalar_heads=0):
             h1 = h0 % GROUP_HEADS
@@ -281,7 +271,8 @@ def tile_mlaattention_pb_kernel(tc, hidden_states, Wkva, Wkvb, k_full, v):
             from_head = wb_raw[:, h0 // GROUP_HEADS].rearrange("p t (h d) -> p t h d", h=GROUP_HEADS)[
                 :, :, h1 : h1 + heads, first : first + size
             ].rearrange("p t h (c i) -> p h c t i", i=RUN)
-            nc.vector.tensor_copy(out=by_head[:, :split], in_=from_head[:, :split])
+            if split:
+                nc.vector.tensor_copy(out=by_head[:, :split], in_=from_head[:, :split])
             if scalar_heads:
                 nc.scalar.copy(out=by_head[:, split:], in_=from_head[:, split:])
             return grouped
@@ -302,7 +293,7 @@ def tile_mlaattention_pb_kernel(tc, hidden_states, Wkva, Wkvb, k_full, v):
             return slice(hf * HALF_TOKENS, (hf + 1) * HALF_TOKENS)
 
         def copy_ckv(copy, hf, m):
-            copy(out=ckv_rows[:, m, half_of(hf)], in_=ckv_acc[hf][m][:])
+            copy(out=ckv_rows[:, m, half_of(hf)], in_=ckv_acc[hf, m][:])
 
         def regroup_ckv(hf):
             regroup(nc.vector.tensor_copy, ckv_grouped[:, half_of(hf), :], ckv_rows[:, :, half_of(hf)])
@@ -312,24 +303,59 @@ def tile_mlaattention_pb_kernel(tc, hidden_states, Wkva, Wkvb, k_full, v):
                 nc, ckv_codes[:, half_of(hf)], ckv_scales[:, half_of(hf)], ckv_grouped[:, half_of(hf), :]
             )
 
-        regroup_wr(nc.scalar.copy, 0)
-        regroup_wr(nc.scalar.copy, 1)
-        regroup_wr(nc.scalar.copy, 2)
+        pair = {}
+        wa = {}
+        transposes(0)
+        pair[0, 0] = x_pair()
+        copy_x(nc.vector.tensor_copy, 0, 0, pair[0, 0])
+        copy_x(nc.scalar.copy, 0, 1, pair[0, 0])
+        pair[0, 1] = x_pair()
+        copy_x(nc.vector.tensor_copy, 0, 2, pair[0, 1])
+        copy_x(nc.scalar.copy, 0, 3, pair[0, 1])
+        quantise_x(0, 0, pair[0, 0])
+        wa[0] = regroup_wa(0, 384)
+        regroup_wr(nc.vector.tensor_copy, 0)
+        quantise_x(0, 2, pair[0, 1])
+        quantise_wa(0, wa[0])
+        sines()
+        transposes(1)
+        first_matmul(0, 0)
+        pair[1, 0] = x_pair()
+        copy_x(nc.scalar.copy, 1, 0, pair[1, 0])
+        copy_x(nc.vector.tensor_copy, 1, 1, pair[1, 0])
+        pair[1, 1] = x_pair()
+        copy_x(nc.scalar.copy, 1, 2, pair[1, 1])
+        wa[1] = regroup_wa(1, 320)
+        copy_x(nc.scalar.copy, 1, 3, pair[1, 1])
+        quantise_x(1, 0, pair[1, 0])
+        quantise_wa(1, wa[1])
+        first_matmul(1, 0)
+        first_matmul(0, 1)
+        first_matmul(1, 1)
+        wa[2] = regroup_wa(2, 192)
+        quantise_x(1, 2, pair[1, 1])
+        wa[3] = regroup_wa(3, 320)
+        quantise_wa(2, wa[2])
+        quantise_wa(3, wa[3])
+        first_matmul(0, 2)
+        first_matmul(0, 3)
+        first_matmul(1, 2)
+        first_matmul(1, 3)
         regroup_wr(nc.scalar.copy, 3)
-        first_values = regroup_weights(0, STEPS[0][2], ND, VD, 0)
-        weights = quantise_weights(first_values)
-        quantise_rope_weights()
+        regroup_wr(nc.scalar.copy, 2)
+        first_values = regroup_weights(0, STEPS[0][2], ND, VD, 1)
         copy_ckv(nc.scalar.copy, 0, 0)
         copy_ckv(nc.scalar.copy, 0, 1)
         copy_ckv(nc.scalar.copy, 0, 2)
-        copy_ckv(nc.scalar.copy, 0, 3)
+        copy_ckv(nc.vector.tensor_copy, 0, 3)
+        weights = quantise_weights(first_values)
         regroup_ckv(0)
-        quantise_ckv(0)
         copy_ckv(nc.scalar.copy, 1, 0)
-        copy_ckv(nc.scalar.copy, 1, 1)
+        copy_ckv(nc.vector.tensor_copy, 1, 1)
         copy_ckv(nc.scalar.copy, 1, 2)
         copy_ckv(nc.scalar.copy, 1, 3)
-        sines()
+        quantise_ckv(0)
+        regroup_wr(nc.vector.tensor_copy, 1)
         regroup_ckv(1)
         quantise_ckv(1)
 
@@ -398,12 +424,12 @@ def tile_mlaattention_pb_kernel(tc, hidden_states, Wkva, Wkvb, k_full, v):
                 k_ps.append(ps)
             return k_ps
 
-        def key_rows(h0, k_ps):
+        def key_rows(h0, k_ps, copies):
             k_out = k_rows[h0 // K_HEADS % K_BUFS]
             h1 = h0 % GROUP_HEADS
-            for hf in range(HALVES):
+            for hf, copy in enumerate(copies):
                 half_chunks = slice(hf * HALF_CHUNKS, (hf + 1) * HALF_CHUNKS)
-                nc.scalar.copy(
+                copy(
                     out=k_out[:, :, half_chunks, 0:ND].rearrange("p h e d -> p e h d"),
                     in_=k_ps[hf][:].rearrange("p e (h d) -> p e h d", h=GROUP_HEADS)[
                         :, :, h1 : h1 + K_HEADS
@@ -415,14 +441,14 @@ def tile_mlaattention_pb_kernel(tc, hidden_states, Wkva, Wkvb, k_full, v):
                     in_=k_out[b:P:B].rearrange("p h c d -> p h (c d)"),
                 )
 
-        def value_group(h0, heads, weights, last_copy):
+        def value_group(h0, heads, weights, copies):
             v_out = outs.tile([P, heads, CHUNKS, VD], F32, tag="v_out%d" % heads)
             per_bank = GROUP_HEADS // heads
             for c in range(0, CHUNKS, per_bank):
                 v_ps = banks.tile([P, per_bank, heads * VD], F32, tag="bank")
                 for e in range(per_bank):
                     second_matmul(v_ps[:, e, :], c + e, weights)
-                copy = last_copy if c + per_bank == CHUNKS else nc.scalar.copy
+                copy = copies[c // per_bank]
                 copy(
                     out=v_out[:, :, c : c + per_bank, :].rearrange("p h e d -> p e h d"),
                     in_=v_ps[:].rearrange("p e (h d) -> p e h d", h=heads),
@@ -434,26 +460,46 @@ def tile_mlaattention_pb_kernel(tc, hidden_states, Wkva, Wkvb, k_full, v):
                 )
 
         kpe_ps = banks.tile([P, CHUNKS, RD], F32, tag="bank")
-        for n, (kind, h0, heads) in enumerate(STEPS):
-            now = weights
-            if n + 1 < len(STEPS):
-                next_kind, next_h0, next_heads = STEPS[n + 1]
-                if next_kind == "v":
-                    weights = quantise_weights(regroup_weights(next_h0, next_heads, ND, VD, 2 if next_heads == GROUP_HEADS else 0))
-                else:
-                    weights = quantise_weights(regroup_weights(next_h0, next_heads, 0, ND))
-                if next_kind == "k" and next_h0 == 0:
-                    rotate(kpe_ps)
-                    lay_k_pe(nc.vector.tensor_copy, 0)
-                    lay_k_pe(nc.vector.tensor_copy, 1)
-            if kind == "v":
-                value_group(h0, heads, now, nc.scalar.copy)
-            else:
-                k_ps = key_matmuls(now)
-                for h in range(h0, h0 + GROUP_HEADS, K_HEADS):
-                    if K_HEADS * 2 <= h < K_HEADS * K_BUFS:
-                        lay_k_pe(nc.vector.tensor_copy, h // K_HEADS)
-                    key_rows(h, k_ps)
-            if n == 0:
-                for c in (0, 1, 2, 3):
-                    k_pe_passes(kpe_ps, c)
+        grouped = {}
+        ready = {0: weights}
+        grouped[3] = regroup_weights(0, 4, 0, ND, 4)
+        grouped[1] = regroup_weights(4, 2, ND, VD, 1)
+        quantise_rope_weights()
+        value_group(0, 4, ready[0], (nc.scalar.copy, nc.scalar.copy, nc.scalar.copy, nc.vector.tensor_copy))
+        for c in range(CHUNKS):
+            k_pe_passes(kpe_ps, c)
+        grouped[4] = regroup_weights(4, 4, 0, ND, 4)
+        ready[1] = quantise_weights(grouped[1])
+        value_group(4, 2, ready[1], (nc.scalar.copy, nc.scalar.copy))
+        grouped[2] = regroup_weights(6, 2, ND, VD, 0)
+        ready[2] = quantise_weights(grouped[2])
+        value_group(6, 2, ready[2], (nc.scalar.copy, nc.scalar.copy))
+        ready[3] = quantise_weights(grouped[3])
+        rotate(kpe_ps)
+        lay_k_pe(nc.vector.tensor_copy, 0)
+        k_ps = key_matmuls(ready[3])
+        key_rows(0, k_ps, (nc.scalar.copy, nc.scalar.copy))
+        lay_k_pe(nc.scalar.copy, 1)
+        key_rows(2, k_ps, (nc.scalar.copy, nc.scalar.copy))
+        ready[4] = quantise_weights(grouped[4])
+        k_ps = key_matmuls(ready[4])
+        lay_k_pe(nc.scalar.copy, 2)
+        key_rows(4, k_ps, (nc.scalar.copy, nc.scalar.copy))
+        lay_k_pe(nc.vector.tensor_copy, 3)
+        key_rows(6, k_ps, (nc.scalar.copy, nc.scalar.copy))
+        grouped[5] = regroup_weights(8, 4, ND, VD, 0)
+        ready[5] = quantise_weights(grouped[5])
+        grouped[6] = regroup_weights(8, 4, 0, ND, 0)
+        value_group(8, 4, ready[5], (nc.scalar.copy, nc.scalar.copy, nc.scalar.copy, nc.scalar.copy))
+        grouped[7] = regroup_weights(12, 4, ND, VD, 0)
+        ready[6] = quantise_weights(grouped[6])
+        k_ps = key_matmuls(ready[6])
+        key_rows(8, k_ps, (nc.scalar.copy, nc.scalar.copy))
+        key_rows(10, k_ps, (nc.scalar.copy, nc.scalar.copy))
+        ready[7] = quantise_weights(grouped[7])
+        grouped[8] = regroup_weights(12, 4, 0, ND, 0)
+        value_group(12, 4, ready[7], (nc.scalar.copy, nc.vector.tensor_copy, nc.scalar.copy, nc.vector.tensor_copy))
+        ready[8] = quantise_weights(grouped[8])
+        k_ps = key_matmuls(ready[8])
+        key_rows(12, k_ps, (nc.scalar.copy, nc.scalar.copy))
+        key_rows(14, k_ps, (nc.scalar.copy, nc.scalar.copy))

@@ -133,14 +133,15 @@ def tile_mlaattention_pb_kernel(tc, hidden_states, Wkva, Wkvb, k_full, v):
         ratio = ROPE_THETA ** (-2.0 / RD)
         width = 1
         while width < HALF:
-            nc.vector.tensor_scalar(
-                out=turns[:, 1, :, width : 2 * width],
-                in0=turns[:, 1, :, 0:width],
-                scalar1=ratio**width,
-                scalar2=None,
-                op0=ALU.mult,
-            )
-            width *= 2
+            for i in range(width, 4 * width, width):
+                nc.vector.tensor_scalar(
+                    out=turns[:, 1, :, i : i + width],
+                    in0=turns[:, 1, :, 0:width],
+                    scalar1=ratio**i,
+                    scalar2=None,
+                    op0=ALU.mult,
+                )
+            width *= 4
         nc.vector.tensor_scalar(
             out=turns[:, 0], in0=turns[:, 1], scalar1=0.25, scalar2=None, op0=ALU.add
         )
@@ -305,6 +306,7 @@ def tile_mlaattention_pb_kernel(tc, hidden_states, Wkva, Wkvb, k_full, v):
 
         pair = {}
         wa = {}
+        grouped = {}
         transposes(0)
         pair[0, 0] = x_pair()
         copy_x(nc.vector.tensor_copy, 0, 0, pair[0, 0])
@@ -345,18 +347,18 @@ def tile_mlaattention_pb_kernel(tc, hidden_states, Wkva, Wkvb, k_full, v):
         regroup_wr(nc.scalar.copy, 2)
         first_values = regroup_weights(0, STEPS[0][2], ND, VD, 1)
         copy_ckv(nc.scalar.copy, 0, 0)
-        copy_ckv(nc.scalar.copy, 0, 1)
+        copy_ckv(nc.vector.tensor_copy, 0, 1)
         copy_ckv(nc.scalar.copy, 0, 2)
         copy_ckv(nc.vector.tensor_copy, 0, 3)
-        weights = quantise_weights(first_values)
         regroup_ckv(0)
         copy_ckv(nc.scalar.copy, 1, 0)
-        copy_ckv(nc.vector.tensor_copy, 1, 1)
+        copy_ckv(nc.scalar.copy, 1, 1)
         copy_ckv(nc.scalar.copy, 1, 2)
         copy_ckv(nc.scalar.copy, 1, 3)
+        weights = quantise_weights(first_values)
         quantise_ckv(0)
-        regroup_wr(nc.vector.tensor_copy, 1)
         regroup_ckv(1)
+        regroup_wr(nc.vector.tensor_copy, 1)
         quantise_ckv(1)
 
         def second_matmul(out, c, weights):
@@ -460,7 +462,6 @@ def tile_mlaattention_pb_kernel(tc, hidden_states, Wkva, Wkvb, k_full, v):
                 )
 
         kpe_ps = banks.tile([P, CHUNKS, RD], F32, tag="bank")
-        grouped = {}
         ready = {0: weights}
         grouped[3] = regroup_weights(0, 4, 0, ND, 4)
         grouped[1] = regroup_weights(4, 2, ND, VD, 1)

@@ -87,10 +87,10 @@ def tile_mlaattention_pb_kernel(tc, hidden_states, Wkva, Wkvb, k_full, v):
                 ),
             )
 
-        load_x(0)
         load_wa(0)
-        load_x(1)
+        load_x(0)
         load_wa(1)
+        load_x(1)
         load_wa(2)
         load_wa(3)
         wb_raw = keep.tile([P, GROUPS, PACK, GROUP_COLS], BF16)
@@ -263,6 +263,23 @@ def tile_mlaattention_pb_kernel(tc, hidden_states, Wkva, Wkvb, k_full, v):
                     stop=(g == PASSES - 1),
                 )
 
+        def first_matmul_chunk(c):
+            hf, e = divmod(c, HALF_CHUNKS)
+            tokens = slice(e * P, (e + 1) * P)
+            ckv_acc[c] = banks.tile([P, PACK, P], F32, tag="bank", name="ckv_chunk%d" % c)
+            for m in range(PACK):
+                latent = slice(m * P, (m + 1) * P)
+                for g in range(PASSES):
+                    nc.tensor.matmul_mx(
+                        out=ckv_acc[c][:, m, :],
+                        lhsT=wa_codes[:, g, latent].bitcast(FP8X4),
+                        lhsT_scale=wa_scales[:, g, latent],
+                        rhs=x_codes[:, hf, g, tokens].bitcast(FP8X4),
+                        rhs_scale=x_scales[:, hf, g, tokens],
+                        start=(g == 0),
+                        stop=(g == PASSES - 1),
+                    )
+
         def regroup_weights(h0, heads, first, size, scalar_heads=0):
             h1 = h0 % GROUP_HEADS
             split = heads - scalar_heads
@@ -304,61 +321,73 @@ def tile_mlaattention_pb_kernel(tc, hidden_states, Wkva, Wkvb, k_full, v):
                 nc, ckv_codes[:, half_of(hf)], ckv_scales[:, half_of(hf)], ckv_grouped[:, half_of(hf), :]
             )
 
+        def chunk_of(c):
+            return slice(c * P, (c + 1) * P)
+
+        def copy_ckv_chunk(copy, c):
+            copy(out=ckv_grouped[:, chunk_of(c), :], in_=ckv_acc[c][:].rearrange("p m n -> p n m"))
+
+        def quantise_ckv_chunk(c):
+            quantise(
+                nc, ckv_codes[:, chunk_of(c)], ckv_scales[:, chunk_of(c)], ckv_grouped[:, chunk_of(c), :]
+            )
+
         pair = {}
         wa = {}
         grouped = {}
-        transposes(0)
-        pair[0, 0] = x_pair()
-        copy_x(nc.vector.tensor_copy, 0, 0, pair[0, 0])
-        copy_x(nc.scalar.copy, 0, 1, pair[0, 0])
-        pair[0, 1] = x_pair()
-        copy_x(nc.vector.tensor_copy, 0, 2, pair[0, 1])
-        copy_x(nc.scalar.copy, 0, 3, pair[0, 1])
-        quantise_x(0, 0, pair[0, 0])
         wa[0] = regroup_wa(0, 384)
         regroup_wr(nc.vector.tensor_copy, 0)
-        quantise_x(0, 2, pair[0, 1])
         quantise_wa(0, wa[0])
         sines()
+        transposes(0)
+        pair[0, 0] = x_pair()
+        copy_x(nc.scalar.copy, 0, 0, pair[0, 0])
+        copy_x(nc.vector.tensor_copy, 0, 1, pair[0, 0])
+        pair[0, 1] = x_pair()
+        copy_x(nc.vector.tensor_copy, 0, 2, pair[0, 1])
+        wa[1] = regroup_wa(1, 320)
+        copy_x(nc.scalar.copy, 0, 3, pair[0, 1])
+        quantise_x(0, 0, pair[0, 0])
+        quantise_wa(1, wa[1])
+        quantise_x(0, 2, pair[0, 1])
+        regroup_wr(nc.scalar.copy, 1)
         transposes(1)
-        first_matmul(0, 0)
         pair[1, 0] = x_pair()
         copy_x(nc.scalar.copy, 1, 0, pair[1, 0])
         copy_x(nc.vector.tensor_copy, 1, 1, pair[1, 0])
         pair[1, 1] = x_pair()
         copy_x(nc.scalar.copy, 1, 2, pair[1, 1])
-        wa[1] = regroup_wa(1, 320)
         copy_x(nc.scalar.copy, 1, 3, pair[1, 1])
         quantise_x(1, 0, pair[1, 0])
-        quantise_wa(1, wa[1])
-        first_matmul(1, 0)
-        first_matmul(0, 1)
-        first_matmul(1, 1)
-        wa[2] = regroup_wa(2, 192)
+        wa[2] = regroup_wa(2, 320)
         quantise_x(1, 2, pair[1, 1])
         wa[3] = regroup_wa(3, 320)
         quantise_wa(2, wa[2])
         quantise_wa(3, wa[3])
+        first_matmul(0, 0)
+        first_matmul(0, 1)
+        first_matmul(1, 0)
+        first_matmul(1, 1)
         first_matmul(0, 2)
         first_matmul(0, 3)
         first_matmul(1, 2)
         first_matmul(1, 3)
-        regroup_wr(nc.scalar.copy, 3)
         regroup_wr(nc.scalar.copy, 2)
-        first_values = regroup_weights(0, STEPS[0][2], ND, VD, 1)
-        copy_ckv(nc.scalar.copy, 0, 0)
-        copy_ckv(nc.vector.tensor_copy, 0, 1)
-        copy_ckv(nc.scalar.copy, 0, 2)
-        copy_ckv(nc.vector.tensor_copy, 0, 3)
+        first_values = regroup_weights(0, STEPS[0][2], ND, VD, 2)
+        copy_ckv(nc.vector.tensor_copy, 0, 0)
+        copy_ckv(nc.vector.tensor_copy, 0, 2)
+        copy_ckv(nc.scalar.copy, 0, 1)
+        copy_ckv(nc.scalar.copy, 0, 3)
+        weights = quantise_weights(first_values)
         regroup_ckv(0)
         copy_ckv(nc.scalar.copy, 1, 0)
         copy_ckv(nc.scalar.copy, 1, 1)
         copy_ckv(nc.scalar.copy, 1, 2)
         copy_ckv(nc.scalar.copy, 1, 3)
-        weights = quantise_weights(first_values)
+        grouped[1] = regroup_weights(4, 2, ND, VD, 1)
         quantise_ckv(0)
         regroup_ckv(1)
-        regroup_wr(nc.vector.tensor_copy, 1)
+        regroup_wr(nc.scalar.copy, 3)
         quantise_ckv(1)
 
         def second_matmul(out, c, weights):
@@ -463,16 +492,15 @@ def tile_mlaattention_pb_kernel(tc, hidden_states, Wkva, Wkvb, k_full, v):
 
         kpe_ps = banks.tile([P, CHUNKS, RD], F32, tag="bank")
         ready = {0: weights}
-        grouped[3] = regroup_weights(0, 4, 0, ND, 4)
-        grouped[1] = regroup_weights(4, 2, ND, VD, 1)
         quantise_rope_weights()
-        value_group(0, 4, ready[0], (nc.scalar.copy, nc.scalar.copy, nc.scalar.copy, nc.vector.tensor_copy))
+        value_group(0, 4, ready[0], (nc.scalar.copy, nc.vector.tensor_copy, nc.scalar.copy, nc.scalar.copy))
         for c in range(CHUNKS):
             k_pe_passes(kpe_ps, c)
-        grouped[4] = regroup_weights(4, 4, 0, ND, 4)
         ready[1] = quantise_weights(grouped[1])
+        grouped[4] = regroup_weights(4, 4, 0, ND, 4)
         value_group(4, 2, ready[1], (nc.scalar.copy, nc.scalar.copy))
         grouped[2] = regroup_weights(6, 2, ND, VD, 0)
+        grouped[3] = regroup_weights(0, 4, 0, ND, 0)
         ready[2] = quantise_weights(grouped[2])
         value_group(6, 2, ready[2], (nc.scalar.copy, nc.scalar.copy))
         ready[3] = quantise_weights(grouped[3])
@@ -484,23 +512,23 @@ def tile_mlaattention_pb_kernel(tc, hidden_states, Wkva, Wkvb, k_full, v):
         key_rows(2, k_ps, (nc.scalar.copy, nc.scalar.copy))
         ready[4] = quantise_weights(grouped[4])
         k_ps = key_matmuls(ready[4])
-        lay_k_pe(nc.scalar.copy, 2)
-        key_rows(4, k_ps, (nc.scalar.copy, nc.scalar.copy))
-        lay_k_pe(nc.vector.tensor_copy, 3)
-        key_rows(6, k_ps, (nc.scalar.copy, nc.scalar.copy))
-        grouped[5] = regroup_weights(8, 4, ND, VD, 0)
-        ready[5] = quantise_weights(grouped[5])
         grouped[6] = regroup_weights(8, 4, 0, ND, 0)
-        value_group(8, 4, ready[5], (nc.scalar.copy, nc.scalar.copy, nc.scalar.copy, nc.scalar.copy))
+        grouped[5] = regroup_weights(8, 4, ND, VD, 3)
+        lay_k_pe(nc.vector.tensor_copy, 2)
+        key_rows(4, k_ps, (nc.scalar.copy, nc.scalar.copy))
+        lay_k_pe(nc.scalar.copy, 3)
+        key_rows(6, k_ps, (nc.scalar.copy, nc.scalar.copy))
+        ready[5] = quantise_weights(grouped[5])
+        value_group(8, 4, ready[5], (nc.vector.tensor_copy, nc.vector.tensor_copy, nc.scalar.copy, nc.scalar.copy))
         grouped[7] = regroup_weights(12, 4, ND, VD, 0)
         ready[6] = quantise_weights(grouped[6])
         k_ps = key_matmuls(ready[6])
         key_rows(8, k_ps, (nc.scalar.copy, nc.scalar.copy))
         key_rows(10, k_ps, (nc.scalar.copy, nc.scalar.copy))
+        grouped[8] = regroup_weights(12, 4, 0, ND, 4)
         ready[7] = quantise_weights(grouped[7])
-        grouped[8] = regroup_weights(12, 4, 0, ND, 0)
-        value_group(12, 4, ready[7], (nc.scalar.copy, nc.vector.tensor_copy, nc.scalar.copy, nc.vector.tensor_copy))
         ready[8] = quantise_weights(grouped[8])
+        value_group(12, 4, ready[7], (nc.scalar.copy, nc.scalar.copy, nc.vector.tensor_copy, nc.scalar.copy))
         k_ps = key_matmuls(ready[8])
         key_rows(12, k_ps, (nc.scalar.copy, nc.scalar.copy))
         key_rows(14, k_ps, (nc.scalar.copy, nc.scalar.copy))

@@ -345,7 +345,7 @@ def tile_mlaattention_pb_kernel(tc, hidden_states, Wkva, Wkvb, k_full, v):
         copy_x(nc.vector.tensor_copy, 0, 1, pair[0, 0])
         pair[0, 1] = x_pair()
         copy_x(nc.vector.tensor_copy, 0, 2, pair[0, 1])
-        wa[1] = regroup_wa(1, 320)
+        wa[1] = regroup_wa(1, 256)
         copy_x(nc.scalar.copy, 0, 3, pair[0, 1])
         quantise_x(0, 0, pair[0, 0])
         quantise_wa(1, wa[1])
@@ -361,7 +361,7 @@ def tile_mlaattention_pb_kernel(tc, hidden_states, Wkva, Wkvb, k_full, v):
         quantise_x(1, 0, pair[1, 0])
         wa[2] = regroup_wa(2, 320)
         quantise_x(1, 2, pair[1, 1])
-        wa[3] = regroup_wa(3, 320)
+        wa[3] = regroup_wa(3, 256)
         quantise_wa(2, wa[2])
         quantise_wa(3, wa[3])
         first_matmul(0, 0)
@@ -493,13 +493,12 @@ def tile_mlaattention_pb_kernel(tc, hidden_states, Wkva, Wkvb, k_full, v):
         kpe_ps = banks.tile([P, CHUNKS, RD], F32, tag="bank")
         ready = {0: weights}
         quantise_rope_weights()
-        value_group(0, 4, ready[0], (nc.scalar.copy, nc.vector.tensor_copy, nc.scalar.copy, nc.scalar.copy))
+        value_group(0, 4, ready[0], (nc.scalar.copy, nc.scalar.copy, nc.scalar.copy, nc.vector.tensor_copy))
         for c in range(CHUNKS):
             k_pe_passes(kpe_ps, c)
         ready[1] = quantise_weights(grouped[1])
-        grouped[4] = regroup_weights(4, 4, 0, ND, 4)
+        grouped[2] = regroup_weights(6, 2, ND, VD, 2)
         value_group(4, 2, ready[1], (nc.scalar.copy, nc.scalar.copy))
-        grouped[2] = regroup_weights(6, 2, ND, VD, 0)
         grouped[3] = regroup_weights(0, 4, 0, ND, 0)
         ready[2] = quantise_weights(grouped[2])
         value_group(6, 2, ready[2], (nc.scalar.copy, nc.scalar.copy))
@@ -508,8 +507,9 @@ def tile_mlaattention_pb_kernel(tc, hidden_states, Wkva, Wkvb, k_full, v):
         lay_k_pe(nc.vector.tensor_copy, 0)
         k_ps = key_matmuls(ready[3])
         key_rows(0, k_ps, (nc.scalar.copy, nc.scalar.copy))
-        lay_k_pe(nc.scalar.copy, 1)
+        lay_k_pe(nc.vector.tensor_copy, 1)
         key_rows(2, k_ps, (nc.scalar.copy, nc.scalar.copy))
+        grouped[4] = regroup_weights(4, 4, 0, ND, 2)
         ready[4] = quantise_weights(grouped[4])
         k_ps = key_matmuls(ready[4])
         grouped[6] = regroup_weights(8, 4, 0, ND, 0)

import math
from contextlib import ExitStack

import concourse.mybir as mybir
from concourse.masks import make_identity

F32 = mybir.dt.float32
BF16 = mybir.dt.bfloat16
I32 = mybir.dt.int32
U32 = mybir.dt.uint32
U8 = mybir.dt.uint8
FP8X4 = mybir.dt.float8_e4m3fn_x4
ALU = mybir.AluOpType
ACT = mybir.ActivationFunctionType

P = 128
PACK = 4
K_PASS = P * PACK

B, S, D, H = 2, 256, 2048, 16
KVL, RD, ND, VD = 512, 128, 64, 128
ROPE_THETA = 10000.0

TOKENS = B * S
CHUNKS = TOKENS // P
HALVES = 2
HALF_CHUNKS = CHUNKS // HALVES
HALF_TOKENS = HALF_CHUNKS * P
PASSES = D // K_PASS
WA_COLS = KVL + RD
HEAD_COLS = ND + VD
GROUP_HEADS = 4
GROUPS = H // GROUP_HEADS
STEPS = (("v", 0, 4), ("v", 4, 2), ("v", 6, 2), ("k", 0, 4), ("k", 4, 4), ("v", 8, 4), ("k", 8, 4), ("v", 12, 4), ("k", 12, 4))
K_HEADS = 2
K_BUFS = 4
GROUP_COLS = GROUP_HEADS * HEAD_COLS
HALF = RD // 2
RUN = 8
ROUND_MAGIC = 1.5 * 2.0**23

FLOPS = 2 * TOKENS * D * WA_COLS + 2 * TOKENS * KVL * H * HEAD_COLS


def regroup(copy, grouped, rows):
    copy(
        out=grouped.rearrange("p (c i) t -> p c t i", i=RUN),
        in_=rows.rearrange("p t (c i) -> p c t i", i=RUN),
    )


def quantise(nc, codes, scales, grouped):
    nc.vector.quantize_mx(
        out=codes.bitcast(FP8X4),
        scales=scales,
        in_=grouped.rearrange("p w t -> p (w t)"),
    )


def tile_mlaattention_pb_kernel(tc, hidden_states, Wkva, Wkvb, k_full, v):
    nc = tc.nc
    with ExitStack() as stack:
        keep = stack.enter_context(tc.tile_pool(name="keep", bufs=1))
        stage = stack.enter_context(tc.tile_pool(name="stage", bufs=3))
        x_stage = stack.enter_context(tc.tile_pool(name="x_stage", bufs=4))
        per_group = stack.enter_context(tc.tile_pool(name="per_group", bufs=4))
        outs = stack.enter_context(tc.tile_pool(name="outs", bufs=3))
        banks = stack.enter_context(tc.psum_pool(name="banks", bufs=8))
        stack.enter_context(tc.manual_schedule())

        x_sb = [keep.tile([P, D], BF16, name="x_sb%d" % c) for c in range(CHUNKS)]
        wa_raw = keep.tile([P, PASSES, 2, 2 * WA_COLS], BF16)

        def load_x(hf):
            for c in range(hf * HALF_CHUNKS, (hf + 1) * HALF_CHUNKS):
                for b in range(B):
                    nc.sync.dma_start(
                        out=x_sb[c][b:P:B],
                        in_=hidden_states[b].rearrange("(q c) k -> c q k", c=CHUNKS)[c],
                    )

        def load_wa(g):
            nc.sync.dma_start(
                out=wa_raw[:, g],
                in_=Wkva[g * K_PASS : (g + 1) * K_PASS, :].rearrange(
                    "(u q e) c -> q u (e c)", u=2, e=2
                ),
            )

        load_wa(0)
        load_x(0)
        load_wa(1)
        load_x(1)
        load_wa(2)
        load_wa(3)
        wb_raw = keep.tile([P, GROUPS, PACK, GROUP_COLS], BF16)
        for hg in range(GROUPS):
            nc.sync.dma_start(
                out=wb_raw[:, hg],
                in_=Wkvb[:, hg * GROUP_COLS : (hg + 1) * GROUP_COLS].rearrange(
                    "(t p) n -> p t n", p=P
                ),
            )

        first_pos = keep.tile([P, 1], I32)
        nc.gpsimd.iota(first_pos[:], pattern=[[0, 1]], base=0, channel_multiplier=1)
        chunk_no = keep.tile([P, CHUNKS], I32)
        nc.gpsimd.iota(chunk_no[:], pattern=[[1, CHUNKS]], base=0, channel_multiplier=0)
        ident = keep.tile([P, P], F32)
        make_identity(nc, ident[:])
        sin_warm = keep.tile([P, 1], F32)
        nc.gpsimd.memset(sin_warm[:], 0.0)
        nc.scalar.activation(out=sin_warm[:], in_=sin_warm[:], func=ACT.Sin)
        nc.vector.tensor_scalar(
            out=first_pos[:],
            in0=first_pos[:],
            scalar1=1,
            scalar2=2,
            op0=ALU.logical_shift_right,
            op1=ALU.logical_shift_left,
        )
        first_pos_f = keep.tile([P, 1], F32)
        nc.vector.tensor_copy(out=first_pos_f[:], in_=first_pos[:])
        turns = keep.tile([P, 2, CHUNKS, HALF], F32)
        nc.vector.tensor_scalar(
            out=turns[:, 1, :, 0:1],
            in0=chunk_no[:].unsqueeze(2),
            scalar1=first_pos_f[:, 0:1],
            scalar2=1.0 / (2.0 * math.pi),
            op0=ALU.add,
            op1=ALU.mult,
        )
        ratio = ROPE_THETA ** (-2.0 / RD)
        width = 1
        while width < HALF:
            for i in range(width, 4 * width, width):
                nc.vector.tensor_scalar(
                    out=turns[:, 1, :, i : i + width],
                    in0=turns[:, 1, :, 0:width],
                    scalar1=ratio**i,
                    scalar2=None,
                    op0=ALU.mult,
                )
            width *= 4
        nc.vector.tensor_scalar(
            out=turns[:, 0], in0=turns[:, 1], scalar1=0.25, scalar2=None, op0=ALU.add
        )
        whole = keep.tile([P, 2, CHUNKS, HALF], F32)
        nc.vector.tensor_scalar(
            out=whole[:],
            in0=turns[:],
            scalar1=ROUND_MAGIC,
            scalar2=ROUND_MAGIC,
            op0=ALU.add,
            op1=ALU.subtract,
        )
        nc.vector.tensor_tensor(out=whole[:], in0=turns[:], in1=whole[:], op=ALU.subtract)
        cos_sin = keep.tile([P, 2, CHUNKS, HALF, 2], F32)

        def sines():
            two_pi = 2.0 * math.pi
            nc.scalar.activation(
                out=cos_sin[:, 0],
                in_=whole[:, 0].unsqueeze(3).to_broadcast([P, CHUNKS, HALF, 2]),
                func=ACT.Sin,
                scale=two_pi,
            )
            for j, sign in enumerate((-1.0, 1.0)):
                nc.scalar.activation(
                    out=cos_sin[:, 1, :, :, j], in_=whole[:, 1], func=ACT.Sin, scale=sign * two_pi
                )

        xt_banks = {}

        def transposes(hf):
            for g in range(PASSES):
                xt_banks[hf, g] = banks.tile([P, 2, HALF_TOKENS], F32, tag="bank", name="xt%d%d" % (hf, g))
            for e in range(HALF_CHUNKS):
                for g in range(PASSES):
                    for u in range(2):
                        first = (2 * g + u) * P
                        nc.tensor.transpose(
                            out=xt_banks[hf, g][:, u, e * P : (e + 1) * P],
                            in_=x_sb[hf * HALF_CHUNKS + e][:].bitcast(F32)[:, first : first + P],
                            identity=ident[:],
                        )

        x_codes = keep.tile([P, HALVES, PASSES, HALF_TOKENS], U32, align_bytes=64)
        x_scales = keep.tile([P, HALVES, PASSES, HALF_TOKENS], U8, align_bytes=64)

        def x_pair():
            x_grouped = x_stage.tile([P, 2, HALF_TOKENS, PACK], BF16, align_bytes=64)
            return x_grouped

        def copy_x(copy, hf, g, x_grouped):
            copy(
                out=x_grouped[:, g % 2]
                .rearrange("q w t -> q (w t)")
                .bitcast(F32)
                .rearrange("q (w u) -> q w u", u=2),
                in_=xt_banks[hf, g][:].rearrange("q u w -> q w u"),
            )

        def quantise_x(hf, g, x_grouped):
            quantise(
                nc,
                x_codes[:, hf, g : g + 2].rearrange("p g w -> p (g w)"),
                x_scales[:, hf, g : g + 2].rearrange("p g w -> p (g w)"),
                x_grouped[:].rearrange("p g w t -> p (g w) t"),
            )

        wa_codes = keep.tile([P, PASSES, KVL], U32, align_bytes=64)
        wa_scales = keep.tile([P, PASSES, KVL], U8, align_bytes=64)
        wr_grouped = keep.tile([P, PASSES, RD, PACK], BF16, align_bytes=64)
        wr_codes = keep.tile([P, PASSES, RD], U32, align_bytes=64)
        wr_scales = keep.tile([P, PASSES, RD], U8, align_bytes=64)

        def wa_rows(g):
            return wa_raw[:, g].rearrange("p u (e c) -> p (u e) c", e=2)

        def regroup_wa(g, vector_cols):
            wa_grouped = stage.tile([P, KVL, PACK], BF16, align_bytes=64)
            regroup(
                nc.vector.tensor_copy,
                wa_grouped[:, 0:vector_cols, :],
                wa_rows(g)[:, :, 0:vector_cols],
            )
            regroup(
                nc.scalar.copy,
                wa_grouped[:, vector_cols:, :],
                wa_rows(g)[:, :, vector_cols:KVL],
            )
            return wa_grouped

        def regroup_wr(copy, g):
            regroup(copy, wr_grouped[:, g], wa_rows(g)[:, :, KVL:])

        def quantise_rope_weights():
            quantise(
                nc,
                wr_codes[:].rearrange("p g c -> p (g c)"),
                wr_scales[:].rearrange("p g c -> p (g c)"),
                wr_grouped[:].rearrange("p g c t -> p (g c) t"),
            )

        def quantise_wa(g, wa_grouped):
            quantise(nc, wa_codes[:, g, :], wa_scales[:, g, :], wa_grouped[:])

        ckv_acc = {}

        def first_matmul(hf, g):
            for m in range(PACK):
                if g == 0:
                    ckv_acc[hf, m] = banks.tile([P, HALF_TOKENS], F32, tag="bank", name="ckv_acc%d%d" % (hf, m))
                latent = slice(m * P, (m + 1) * P)
                nc.tensor.matmul_mx(
                    out=ckv_acc[hf, m][:],
                    lhsT=wa_codes[:, g, latent].bitcast(FP8X4),
                    lhsT_scale=wa_scales[:, g, latent],
                    rhs=x_codes[:, hf, g, :].bitcast(FP8X4),
                    rhs_scale=x_scales[:, hf, g, :],
                    start=(g == 0),
                    stop=(g == PASSES - 1),
                )

        def first_matmul_chunk(c):
            hf, e = divmod(c, HALF_CHUNKS)
            tokens = slice(e * P, (e + 1) * P)
            ckv_acc[c] = banks.tile([P, PACK, P], F32, tag="bank", name="ckv_chunk%d" % c)
            for m in range(PACK):
                latent = slice(m * P, (m + 1) * P)
                for g in range(PASSES):
                    nc.tensor.matmul_mx(
                        out=ckv_acc[c][:, m, :],
                        lhsT=wa_codes[:, g, latent].bitcast(FP8X4),
                        lhsT_scale=wa_scales[:, g, latent],
                        rhs=x_codes[:, hf, g, tokens].bitcast(FP8X4),
                        rhs_scale=x_scales[:, hf, g, tokens],
                        start=(g == 0),
                        stop=(g == PASSES - 1),
                    )

        def regroup_weights(h0, heads, first, size, scalar_heads=0):
            h1 = h0 % GROUP_HEADS
            split = heads - scalar_heads
            words = heads * size
            grouped = stage.tile([P, words, PACK], BF16, align_bytes=64, tag="wb%d" % words)
            by_head = grouped[:].rearrange("p (h c i) t -> p h c t i", h=heads, i=RUN)
            from_head = wb_raw[:, h0 // GROUP_HEADS].rearrange("p t (h d) -> p t h d", h=GROUP_HEADS)[
                :, :, h1 : h1 + heads, first : first + size
            ].rearrange("p t h (c i) -> p h c t i", i=RUN)
            if split:
                nc.vector.tensor_copy(out=by_head[:, :split], in_=from_head[:, :split])
            if scalar_heads:
                nc.scalar.copy(out=by_head[:, split:], in_=from_head[:, split:])
            return grouped

        def quantise_weights(grouped):
            words = grouped.shape[1]
            codes = per_group.tile([P, words], U32, align_bytes=64, tag="codes%d" % words)
            scales = per_group.tile([P, words], U8, align_bytes=64, tag="scales%d" % words)
            quantise(nc, codes[:], scales[:], grouped[:])
            return codes, scales

        ckv_rows = keep.tile([P, PACK, TOKENS], BF16)
        ckv_grouped = keep.tile([P, TOKENS, PACK], BF16, align_bytes=64)
        ckv_codes = keep.tile([P, TOKENS], U32, align_bytes=64)
        ckv_scales = keep.tile([P, TOKENS], U8, align_bytes=64)

        def half_of(hf):
            return slice(hf * HALF_TOKENS, (hf + 1) * HALF_TOKENS)

        def copy_ckv(copy, hf, m):
            copy(out=ckv_rows[:, m, half_of(hf)], in_=ckv_acc[hf, m][:])

        def regroup_ckv(hf):
            regroup(nc.vector.tensor_copy, ckv_grouped[:, half_of(hf), :], ckv_rows[:, :, half_of(hf)])

        def quantise_ckv(hf):
            quantise(
                nc, ckv_codes[:, half_of(hf)], ckv_scales[:, half_of(hf)], ckv_grouped[:, half_of(hf), :]
            )

        def chunk_of(c):
            return slice(c * P, (c + 1) * P)

        def copy_ckv_chunk(copy, c):
            copy(out=ckv_grouped[:, chunk_of(c), :], in_=ckv_acc[c][:].rearrange("p m n -> p n m"))

        def quantise_ckv_chunk(c):
            quantise(
                nc, ckv_codes[:, chunk_of(c)], ckv_scales[:, chunk_of(c)], ckv_grouped[:, chunk_of(c), :]
            )

        pair = {}
        wa = {}
        grouped = {}
        wa[0] = regroup_wa(0, 384)
        regroup_wr(nc.vector.tensor_copy, 0)
        quantise_wa(0, wa[0])
        sines()
        transposes(0)
        pair[0, 0] = x_pair()
        copy_x(nc.scalar.copy, 0, 0, pair[0, 0])
        copy_x(nc.vector.tensor_copy, 0, 1, pair[0, 0])
        pair[0, 1] = x_pair()
        copy_x(nc.vector.tensor_copy, 0, 2, pair[0, 1])
        wa[1] = regroup_wa(1, 256)
        copy_x(nc.scalar.copy, 0, 3, pair[0, 1])
        quantise_x(0, 0, pair[0, 0])
        quantise_wa(1, wa[1])
        quantise_x(0, 2, pair[0, 1])
        regroup_wr(nc.scalar.copy, 1)
        transposes(1)
        pair[1, 0] = x_pair()
        copy_x(nc.scalar.copy, 1, 0, pair[1, 0])
        copy_x(nc.vector.tensor_copy, 1, 1, pair[1, 0])
        pair[1, 1] = x_pair()
        copy_x(nc.scalar.copy, 1, 2, pair[1, 1])
        copy_x(nc.scalar.copy, 1, 3, pair[1, 1])
        quantise_x(1, 0, pair[1, 0])
        wa[2] = regroup_wa(2, 320)
        quantise_x(1, 2, pair[1, 1])
        wa[3] = regroup_wa(3, 256)
        quantise_wa(2, wa[2])
        quantise_wa(3, wa[3])
        first_matmul(0, 0)
        first_matmul(0, 1)
        first_matmul(1, 0)
        first_matmul(1, 1)
        first_matmul(0, 2)
        first_matmul(0, 3)
        first_matmul(1, 2)
        first_matmul(1, 3)
        regroup_wr(nc.scalar.copy, 2)
        first_values = regroup_weights(0, STEPS[0][2], ND, VD, 2)
        copy_ckv(nc.vector.tensor_copy, 0, 0)
        copy_ckv(nc.vector.tensor_copy, 0, 2)
        copy_ckv(nc.scalar.copy, 0, 1)
        copy_ckv(nc.scalar.copy, 0, 3)
        weights = quantise_weights(first_values)
        regroup_ckv(0)
        copy_ckv(nc.scalar.copy, 1, 0)
        copy_ckv(nc.scalar.copy, 1, 1)
        copy_ckv(nc.scalar.copy, 1, 2)
        copy_ckv(nc.scalar.copy, 1, 3)
        grouped[1] = regroup_weights(4, 2, ND, VD, 1)
        quantise_ckv(0)
        regroup_ckv(1)
        regroup_wr(nc.scalar.copy, 3)
        quantise_ckv(1)

        def second_matmul(out, c, weights):
            codes, scales = weights
            tokens = slice(c * P, (c + 1) * P)
            nc.tensor.matmul_mx(
                out=out,
                lhsT=ckv_codes[:, tokens].bitcast(FP8X4),
                lhsT_scale=ckv_scales[:, tokens],
                rhs=codes[:].bitcast(FP8X4),
                rhs_scale=scales[:],
                start=True,
                stop=True,
            )

        def k_pe_passes(kpe_ps, c):
            hf, e = divmod(c, HALF_CHUNKS)
            tokens = slice(e * P, (e + 1) * P)
            for g in range(PASSES):
                nc.tensor.matmul_mx(
                    out=kpe_ps[:, c, :],
                    lhsT=x_codes[:, hf, g, tokens].bitcast(FP8X4),
                    lhsT_scale=x_scales[:, hf, g, tokens],
                    rhs=wr_codes[:, g, :].bitcast(FP8X4),
                    rhs_scale=wr_scales[:, g, :],
                    start=(g == 0),
                    stop=(g == PASSES - 1),
                )

        pairs_shape = [P, CHUNKS, HALF, 2]
        by_cos = keep.tile(pairs_shape, F32)
        by_sin = keep.tile(pairs_shape, F32)
        kpe_rot = keep.tile([P, CHUNKS, RD], F32)

        def rotate(kpe_ps):
            pairs = kpe_ps[:].rearrange("p c (i j) -> p c i j", j=2)
            nc.vector.tensor_tensor(out=by_cos[:], in0=pairs, in1=cos_sin[:, 0], op=ALU.mult)
            nc.vector.tensor_tensor(
                out=by_sin[:], in0=pairs[:, :, :, ::-1], in1=cos_sin[:, 1], op=ALU.mult
            )
            nc.vector.tensor_tensor(
                out=kpe_rot[:].rearrange("p c (i j) -> p c i j", j=2),
                in0=by_cos[:],
                in1=by_sin[:],
                op=ALU.add,
            )

        k_rows = [
            keep.tile([P, K_HEADS, CHUNKS, HEAD_COLS], F32, name="k_rows%d" % i)
            for i in range(K_BUFS)
        ]

        def lay_k_pe(copy, i):
            copy(
                out=k_rows[i][:, :, :, ND:],
                in_=kpe_rot[:].unsqueeze(1).to_broadcast([P, K_HEADS, CHUNKS, RD]),
            )

        def key_matmuls(weights):
            k_ps = []
            for hf in range(HALVES):
                ps = banks.tile([P, HALF_CHUNKS, GROUP_HEADS * ND], F32, tag="bank")
                for e in range(HALF_CHUNKS):
                    second_matmul(ps[:, e, :], hf * HALF_CHUNKS + e, weights)
                k_ps.append(ps)
            return k_ps

        def key_rows(h0, k_ps, copies):
            k_out = k_rows[h0 // K_HEADS % K_BUFS]
            h1 = h0 % GROUP_HEADS
            for hf, copy in enumerate(copies):
                half_chunks = slice(hf * HALF_CHUNKS, (hf + 1) * HALF_CHUNKS)
                copy(
                    out=k_out[:, :, half_chunks, 0:ND].rearrange("p h e d -> p e h d"),
                    in_=k_ps[hf][:].rearrange("p e (h d) -> p e h d", h=GROUP_HEADS)[
                        :, :, h1 : h1 + K_HEADS
                    ],
                )
            for b in range(B):
                nc.sync.dma_start(
                    out=k_full[b, h0 : h0 + K_HEADS].rearrange("h (q c) d -> q h (c d)", c=CHUNKS),
                    in_=k_out[b:P:B].rearrange("p h c d -> p h (c d)"),
                )

        def value_group(h0, heads, weights, copies):
            v_out = outs.tile([P, heads, CHUNKS, VD], F32, tag="v_out%d" % heads)
            per_bank = GROUP_HEADS // heads
            for c in range(0, CHUNKS, per_bank):
                v_ps = banks.tile([P, per_bank, heads * VD], F32, tag="bank")
                for e in range(per_bank):
                    second_matmul(v_ps[:, e, :], c + e, weights)
                copy = copies[c // per_bank]
                copy(
                    out=v_out[:, :, c : c + per_bank, :].rearrange("p h e d -> p e h d"),
                    in_=v_ps[:].rearrange("p e (h d) -> p e h d", h=heads),
                )
            for b in range(B):
                nc.sync.dma_start(
                    out=v[b, h0 : h0 + heads].rearrange("h (q c) d -> q h (c d)", c=CHUNKS),
                    in_=v_out[b:P:B].rearrange("p h c d -> p h (c d)"),
                )

        kpe_ps = banks.tile([P, CHUNKS, RD], F32, tag="bank")
        ready = {0: weights}
        quantise_rope_weights()
        value_group(0, 4, ready[0], (nc.scalar.copy, nc.scalar.copy, nc.scalar.copy, nc.vector.tensor_copy))
        for c in range(CHUNKS):
            k_pe_passes(kpe_ps, c)
        ready[1] = quantise_weights(grouped[1])
        grouped[2] = regroup_weights(6, 2, ND, VD, 2)
        value_group(4, 2, ready[1], (nc.scalar.copy, nc.scalar.copy))
        grouped[3] = regroup_weights(0, 4, 0, ND, 0)
        ready[2] = quantise_weights(grouped[2])
        value_group(6, 2, ready[2], (nc.scalar.copy, nc.scalar.copy))
        ready[3] = quantise_weights(grouped[3])
        rotate(kpe_ps)
        lay_k_pe(nc.vector.tensor_copy, 0)
        k_ps = key_matmuls(ready[3])
        key_rows(0, k_ps, (nc.scalar.copy, nc.scalar.copy))
        lay_k_pe(nc.vector.tensor_copy, 1)
        key_rows(2, k_ps, (nc.scalar.copy, nc.scalar.copy))
        grouped[4] = regroup_weights(4, 4, 0, ND, 2)
        ready[4] = quantise_weights(grouped[4])
        k_ps = key_matmuls(ready[4])
        grouped[6] = regroup_weights(8, 4, 0, ND, 0)
        grouped[5] = regroup_weights(8, 4, ND, VD, 3)
        lay_k_pe(nc.vector.tensor_copy, 2)
        key_rows(4, k_ps, (nc.scalar.copy, nc.scalar.copy))
        lay_k_pe(nc.scalar.copy, 3)
        key_rows(6, k_ps, (nc.scalar.copy, nc.scalar.copy))
        ready[5] = quantise_weights(grouped[5])
        value_group(8, 4, ready[5], (nc.vector.tensor_copy, nc.vector.tensor_copy, nc.scalar.copy, nc.scalar.copy))
        grouped[7] = regroup_weights(12, 4, ND, VD, 0)
        ready[6] = quantise_weights(grouped[6])
        k_ps = key_matmuls(ready[6])
        key_rows(8, k_ps, (nc.scalar.copy, nc.scalar.copy))
        key_rows(10, k_ps, (nc.scalar.copy, nc.scalar.copy))
        grouped[8] = regroup_weights(12, 4, 0, ND, 4)
        ready[7] = quantise_weights(grouped[7])
        ready[8] = quantise_weights(grouped[8])
        value_group(12, 4, ready[7], (nc.scalar.copy, nc.scalar.copy, nc.vector.tensor_copy, nc.scalar.copy))
        k_ps = key_matmuls(ready[8])
        key_rows(12, k_ps, (nc.scalar.copy, nc.scalar.copy))
        key_rows(14, k_ps, (nc.scalar.copy, nc.scalar.copy))
